import numpy as np
import ml_dtypes


def mxq(x, axis, fmt="e4m3"):
    dtype, down = {"e4m3": (ml_dtypes.float8_e4m3fn, 7), "e5m2": (ml_dtypes.float8_e5m2, 14)}[fmt]
    v = np.moveaxis(np.asarray(x, np.float32).astype(ml_dtypes.bfloat16).astype(np.float64), axis, -1)
    blocks = v.reshape(v.shape[:-1] + (-1, 32))
    amax = np.abs(blocks).max(-1, keepdims=True)
    byte = np.maximum(np.where(amax > 0, np.frexp(amax)[1] - 1 + 127, 0) - down, 1)
    scale = np.exp2(byte - 127.0)
    codes = (blocks / scale).astype(np.float32).astype(dtype).astype(np.float64)
    return np.moveaxis((codes * scale).reshape(v.shape), -1, axis)


WIDE = False


def mx_kscale(k):
    if not WIDE:
        return np.ones(k)
    levels = np.array([18, -18])
    if k % 512:
        return np.exp2(np.random.permutation(np.resize(levels, k // 32))).repeat(32)
    a = np.empty((k // 512, 16))
    for p in range(k // 512):
        a[p, :8] = np.random.permutation(np.resize(levels, 8))
        for g in range(8):
            far = levels[np.abs(levels - a[p, g]) >= 10]
            a[p, g + 8] = far[np.random.randint(len(far))]
    return np.exp2(a.ravel()).repeat(32)


BF16 = ml_dtypes.bfloat16


def bf(x):
    return np.asarray(x, np.float32).astype(BF16)


def f64(x):
    return np.asarray(x).astype(np.float64)


B, IN, H = 512, 1024, 1024


def sigmoid(v):
    return 1.0 / (1.0 + np.exp(-v))


def setup_inputs():
    s = mx_kscale(B)[:, None]
    u = mx_kscale(H)
    v = mx_kscale(H)
    wsc = np.sqrt(2.0 / (IN + H))
    usc = 1.0 / np.sqrt(H)
    joint_h0 = bf(np.random.standard_normal((B, H)))
    mgn_h = bf(np.random.standard_normal((B, IN)))
    W_r = bf(np.random.standard_normal((IN, H)) * wsc)
    W_h = bf(np.random.standard_normal((IN, H)) * wsc)
    U_r0 = bf(np.random.standard_normal((H, H)) * usc)
    U_h0 = bf(np.random.standard_normal((H, H)) * usc)
    b_r = bf(np.random.standard_normal(H) * 0.5)
    b_h = bf(np.random.standard_normal(H) * 0.5)
    grad_out = bf(np.random.standard_normal((B, H)) * np.exp2(np.random.randint(-6, 1, (B, 1))) * 4.0 / s * np.min(s) * u)
    r = sigmoid(f64(mgn_h) @ f64(W_r) + f64(joint_h0) @ f64(U_r0) + f64(b_r))
    g = f64(joint_h0) * r
    y = np.tanh(f64(mgn_h) @ f64(W_h) + g @ f64(U_h0) + f64(b_h))
    return {"joint_h": bf(f64(joint_h0) * s),
            "mgn_h": mgn_h,
            "W_r": W_r,
            "W_h": W_h,
            "U_r": bf(f64(U_r0) * v[:, None] / v),
            "U_h": bf(f64(U_h0) * v[:, None] / u),
            "b_r": b_r,
            "b_h": b_h,
            "r": np.asarray(r, np.float32),
            "g": np.asarray(g, np.float32),
            "y": np.asarray(y, np.float32),
            "grad_out": grad_out}


def reference(joint_h, mgn_h, W_r, W_h, U_r, U_h, b_r, b_h, r, g, y, grad_out):
    rf, gf, yf = f64(r), f64(g), f64(y)
    dz2 = f64(grad_out) * (1.0 - yf * yf)
    dg = mxq(dz2, 1, "e5m2") @ mxq(f64(U_h), 1, "e4m3").T
    dz1 = dg * gf * (1.0 - rf)
    d_joint_h = (mxq(dz1, 1, "e5m2") @ mxq(f64(U_r), 1, "e4m3").T) + dg * rf
    d_U_r = mxq(f64(joint_h), 0, "e4m3").T @ mxq(dz1, 0, "e5m2")
    return d_joint_h, d_U_r

@@ -1,0 +1,300 @@
+from contextlib import ExitStack
+
+import concourse.mybir as mybir
+from concourse.masks import make_identity
+
+B, H = 512, 1024
+FLOPS = 3 * 2 * B * H * H
+BYTES = 2 * (2 * B * H + 2 * H * H) + 4 * (3 * B * H) + 4 * (B * H + H * H)
+
+F32 = mybir.dt.float32
+BF16 = mybir.dt.bfloat16
+U32 = mybir.dt.uint32
+U8 = mybir.dt.uint8
+E4M3 = mybir.dt.float8_e4m3fn_x4
+E5M2 = mybir.dt.float8_e5m2_x4
+ALU = mybir.AluOpType
+ACT = mybir.ActivationFunctionType
+
+P = 128
+PACK = 4
+HALF = 512
+
+
+def tile_joint_gru_pa_v_kernel(tc, joint_h, mgn_h, W_r, W_h, U_r, U_h, b_r, b_h, r, g, y, grad_out, out_0, out_1):
+    nc = tc.nc
+    with ExitStack() as ctx:
+        keep = ctx.enter_context(tc.tile_pool(name="keep", bufs=1))
+        psum = ctx.enter_context(tc.psum_pool(name="psum", bufs=1))
+        ctx.enter_context(tc.manual_schedule())
+
+        def sb(name, width, dtype, tag="", bufs=1):
+            return keep.tile([P, width], dtype, name=name, tag=tag or name, bufs=bufs, align_bytes=64)
+
+        def slots(t):
+            return t.rearrange("(p j) w -> p j w", j=PACK)
+
+        def cols(h, width=HALF):
+            return slice(h * width, (h + 1) * width)
+
+        def mx_tiles(name, width):
+            return sb(name + "_codes", width, U32), sb(name + "_scales", width, U8)
+
+        def quantize(dst, where, src, fmt):
+            nc.vector.quantize_mx(out=dst[0][:, where].bitcast(fmt), scales=dst[1][:, where], in_=src)
+
+        def matmul(acc, lhs, lhs_cols, lhs_fmt, rhs, rhs_cols, rhs_fmt, start, stop):
+            nc.tensor.matmul_mx(
+                out=acc[:],
+                lhsT=lhs[0][:, lhs_cols].bitcast(lhs_fmt),
+                lhsT_scale=lhs[1][:, lhs_cols],
+                rhs=rhs[0][:, rhs_cols].bitcast(rhs_fmt),
+                rhs_scale=rhs[1][:, rhs_cols],
+                start=start,
+                stop=stop,
+            )
+
+        ident = sb("ident", P, F32)
+        make_identity(nc, ident[:])
+
+        go_sb = [sb("go%d" % j, H, BF16) for j in range(PACK)]
+        y_sb = [sb("y%d" % j, H, F32) for j in range(PACK)]
+        g_sb = [sb("g%d" % j, H, F32) for j in range(PACK)]
+        r_sb = [sb("r%d" % j, H, F32) for j in range(PACK)]
+        jh_sb = sb("jh", PACK * H, BF16)
+        weights = {"h": U_h, "r": U_r}
+        u_sb = {(w, q): sb("u%s%d" % (w, q), 2 * H, BF16) for w in "hr" for q in range(4)}
+
+        dz2_mx = [mx_tiles("dz2_%d" % j, 2 * P) for j in range(PACK)]
+        u_mx = {(w, h, k): mx_tiles("u%s%d%d" % (w, h, k), HALF) for w in "hr" for h in range(2) for k in range(2)}
+        dz1_sb = [sb("dz1_%d" % h, PACK * HALF, BF16) for h in range(2)]
+        dz1_tok = [sb("dz1_tok%d" % h, PACK * HALF, BF16) for h in range(2)]
+        dz1_tok_mx = [mx_tiles("dz1_tok%d" % h, HALF) for h in range(2)]
+        dz1_feat_mx = {(h, jp): mx_tiles("dz1_feat%d%d" % (h, jp), 2 * P) for h in range(2) for jp in range(2)}
+        jh_tok = [sb("jh_tok%d" % h, PACK * HALF, BF16) for h in range(2)]
+        jh_mx = [mx_tiles("jh%d" % h, HALF) for h in range(2)]
+        u_t = {(w, h, k): sb("u_t%s%d%d" % (w, h, k), PACK * HALF, BF16) for w in "hr" for h in range(2) for k in range(2)}
+        staged = {}
+
+        def load_dz2_inputs(j):
+            nc.sync.dma_start(out=y_sb[j][:], in_=slots(y)[:, j, :])
+            nc.sync.dma_start(out=go_sb[j][:], in_=slots(grad_out)[:, j, :])
+
+        def load_y(j):
+            nc.sync.dma_start(out=y_sb[j][:], in_=slots(y)[:, j, :])
+
+        def load_gate(j, h):
+            nc.sync.dma_start(out=g_sb[j][:, cols(h)], in_=slots(g)[:, j, cols(h)])
+            nc.sync.dma_start(out=r_sb[j][:, cols(h)], in_=slots(r)[:, j, cols(h)])
+
+        def load_weight(w, q):
+            rows = weights[w][cols(q, 2 * P), :]
+            nc.sync.dma_start(out=u_sb[w, q][:], in_=rows.rearrange("(p m) k -> p (m k)", m=2))
+
+        def load_jh():
+            nc.sync.dma_start(out=jh_sb[:], in_=joint_h.rearrange("(p j) w -> p (j w)", j=PACK))
+
+        def transpose_pair(name, src_a, src_b):
+            bank = psum.tile([P, 2, 2, P], F32, name=name, tag="bank", bufs=8)
+            for n, src in enumerate((src_a, src_b)):
+                words = src.bitcast(F32)
+                for u in range(2):
+                    nc.tensor.transpose(bank[:, n, u, :], words[:, u : 2 * P : 2], ident[:])
+            return bank
+
+        def square(j):
+            nc.scalar.activation(out=y_sb[j][:], in_=y_sb[j][:], func=ACT.Square)
+
+        def neg_dz2(j):
+            nc.vector.scalar_tensor_tensor(out=go_sb[j][:], in0=y_sb[j][:], scalar=1.0, in1=go_sb[j][:], op0=ALU.subtract, op1=ALU.mult)
+
+        def turn_dz2(j):
+            staged["dz2_bank", j] = transpose_pair("dz2_bank%d" % j, go_sb[j][:, cols(0)], go_sb[j][:, cols(1)])
+
+        def copy_dz2(j, copy):
+            staged["dz2", j] = sb("dz2_t%d" % j, H, BF16)
+            dst = staged["dz2", j][:].bitcast(F32).rearrange("p (k c u) -> p k c u", k=2, u=2)
+            copy(out=dst, in_=staged["dz2_bank", j][:].rearrange("p k u c -> p k c u"))
+
+        def quantize_dz2(j):
+            quantize(dz2_mx[j], slice(None), staged["dz2", j][:], E5M2)
+
+        def turn_weight(w, q, k):
+            src = u_sb[w, q]
+            staged["u_bank", w, q, k] = transpose_pair("u_bank%s%d%d" % (w, q, k), src[:, cols(k)], src[:, cols(2 + k)])
+
+        def copy_weight(w, q, k, copy):
+            h, a = divmod(q, 2)
+            dst = u_t[w, h, k][:, cols(a, H)].bitcast(F32).rearrange("p (c m u) -> p c m u", m=2, u=2)
+            copy(out=dst, in_=staged["u_bank", w, q, k][:].rearrange("p m u c -> p c m u"))
+
+        def quantize_weight(w, h, k):
+            quantize(u_mx[w, h, k], slice(None), u_t[w, h, k][:], E4M3)
+
+        def quantize_weight_part(w, q, k):
+            h, a = divmod(q, 2)
+            quantize(u_mx[w, h, k], cols(a, 2 * P), u_t[w, h, k][:, cols(a, H)], E4M3)
+
+        def product_dg(j, h):
+            staged["dg", j, h] = psum.tile([P, HALF], F32, name="dg%d%d" % (j, h), tag="bank", bufs=8)
+            for k in range(2):
+                matmul(staged["dg", j, h], dz2_mx[j], cols(k, P), E5M2, u_mx["h", h, k], slice(None), E4M3, k == 0, k == 1)
+
+        def gate_factor(j, h):
+            nc.vector.scalar_tensor_tensor(out=g_sb[j][:, cols(h)], in0=r_sb[j][:, cols(h)], scalar=1.0, in1=g_sb[j][:, cols(h)], op0=ALU.subtract, op1=ALU.mult)
+
+        def make_dz1(j, h):
+            nc.vector.tensor_tensor(out=dz1_sb[h][:, cols(j)], in0=staged["dg", j, h][:], in1=g_sb[j][:, cols(h)], op=ALU.mult)
+
+        def make_dg_r(j, h):
+            nc.vector.scalar_tensor_tensor(out=r_sb[j][:, cols(h)], in0=staged["dg", j, h][:], scalar=-1.0, in1=r_sb[j][:, cols(h)], op0=ALU.mult, op1=ALU.mult)
+
+        def interleave(copy, dst, src):
+            copy(out=dst.rearrange("p (c i j) -> p c j i", i=4, j=PACK), in_=src.rearrange("p j (c i) -> p c j i", i=4))
+
+        def interleave_dz1(h, part, copy):
+            src = dz1_sb[h][:].rearrange("p (j c) -> p j c", j=PACK)[:, :, cols(part, 2 * P)]
+            interleave(copy, dz1_tok[h][:, cols(part, H)], src)
+
+        def quantize_dz1_tok(h):
+            quantize(dz1_tok_mx[h], slice(None), dz1_tok[h][:], E5M2)
+
+        def interleave_jh(q, copy):
+            src = jh_sb[:].rearrange("p (j c) -> p j c", j=PACK)[:, :, cols(q, 2 * P)]
+            interleave(copy, jh_tok[q // 2][:, cols(q % 2, H)], src)
+
+        def quantize_jh(h):
+            quantize(jh_mx[h], slice(None), jh_tok[h][:], E4M3)
+
+        def turn_dz1(h, jp):
+            staged["dz1_bank", h, jp] = transpose_pair("dz1_bank%d%d" % (h, jp), dz1_sb[h][:, cols(2 * jp)], dz1_sb[h][:, cols(2 * jp + 1)])
+
+        def copy_dz1(h, jp, copy):
+            staged["dz1", h, jp] = sb("dz1_t%d%d" % (h, jp), H, BF16)
+            dst = staged["dz1", h, jp][:].bitcast(F32).rearrange("p (n c u) -> p n c u", n=2, u=2)
+            copy(out=dst, in_=staged["dz1_bank", h, jp][:].rearrange("p n u c -> p n c u"))
+
+        def quantize_dz1_feat(h, jp):
+            quantize(dz1_feat_mx[h, jp], slice(None), staged["dz1", h, jp][:], E5M2)
+
+        def product_out1(t, h):
+            staged["acc1", t, h] = psum.tile([P, HALF], F32, name="acc1_%d%d" % (t, h), tag="bank", bufs=8)
+            matmul(staged["acc1", t, h], jh_mx[t // 4], cols(t % 4, P), E4M3, dz1_tok_mx[h], slice(None), E5M2, True, True)
+
+        def out1_stage(t, h):
+            return (y_sb, g_sb)[h][t // 2][:, cols(t % 2)]
+
+        def copy_out1(t, h, copy):
+            copy(out=out1_stage(t, h), in_=staged["acc1", t, h][:])
+
+        def store_out1(t, h):
+            nc.sync.dma_start(out=out_1[cols(t, P), cols(h)], in_=out1_stage(t, h))
+
+        def product_out0(j, h):
+            staged["acc0", j, h] = psum.tile([P, HALF], F32, name="acc0_%d%d" % (j, h), tag="bank", bufs=8)
+            for k in range(2):
+                matmul(staged["acc0", j, h], dz1_feat_mx[k, j // 2], cols(j % 2, P), E5M2, u_mx["r", h, k], slice(None), E4M3, k == 0, k == 1)
+
+        def add_out0(j, h):
+            nc.vector.tensor_tensor(out=r_sb[j][:, cols(h)], in0=staged["acc0", j, h][:], in1=r_sb[j][:, cols(h)], op=ALU.add)
+
+        def store_out0(j, h):
+            nc.sync.dma_start(out=slots(out_0)[:, j, cols(h)], in_=r_sb[j][:, cols(h)])
+
+        def warm(n, place):
+            bank = psum.tile([P, P], F32, name="warm", tag="bank", bufs=8)
+            for i in range(n):
+                nc.tensor.matmul(bank[:], ident[:], ident[:], start=True, stop=True)
+
+        on_scalar = nc.scalar.copy
+        on_vector = nc.vector.tensor_copy
+
+        def needs(step):
+            fn, args = step[0], step[1:]
+            if fn == neg_dz2:
+                return [(square,) + args]
+            if fn == turn_dz2:
+                return [(neg_dz2,) + args]
+            if fn == copy_dz2:
+                return [(turn_dz2,) + args]
+            if fn == quantize_dz2:
+                return [(copy_dz2,) + args]
+            if fn == copy_weight:
+                return [(turn_weight,) + args]
+            if fn == quantize_weight_part:
+                return [(copy_weight,) + args]
+            if fn == quantize_weight:
+                w, h, k = args
+                return [(copy_weight, w, 2 * h, k), (copy_weight, w, 2 * h + 1, k)]
+            if fn == product_dg:
+                j, h = args
+                return [(quantize_dz2, j)] + [(quantize_weight_part, "h", 2 * h + a, k) for a in range(2) for k in range(2)]
+            if fn == make_dg_r or fn == make_dz1:
+                return [(product_dg,) + args, (gate_factor,) + args]
+            if fn == interleave_dz1:
+                return [(make_dz1, j, args[0]) for j in range(PACK)]
+            if fn == quantize_dz1_tok:
+                return [(interleave_dz1, args[0], part) for part in range(2)]
+            if fn == quantize_jh:
+                return [(interleave_jh, 2 * args[0] + part) for part in range(2)]
+            if fn == turn_dz1:
+                return [(make_dz1, 2 * args[1] + n, args[0]) for n in range(2)]
+            if fn == copy_dz1:
+                return [(turn_dz1,) + args]
+            if fn == quantize_dz1_feat:
+                return [(copy_dz1,) + args]
+            if fn == product_out1:
+                return [(quantize_jh, args[0] // 4), (quantize_dz1_tok, args[1])]
+            if fn == copy_out1:
+                return [(product_out1,) + args]
+            if fn == store_out1:
+                return [(copy_out1,) + args]
+            if fn == product_out0:
+                j, h = args
+                return [(quantize_dz1_feat, k, j // 2) for k in range(2)] + [(quantize_weight_part, "r", 2 * h + a, k) for a in range(2) for k in range(2)]
+            if fn == add_out0:
+                return [(product_out0,) + args]
+            if fn == store_out0:
+                return [(add_out0,) + args]
+            return []
+
+        def bank_use(step):
+            fn, args = step[0], step[1:]
+            readers = {turn_dz2: [copy_dz2], turn_weight: [copy_weight], turn_dz1: [copy_dz1], product_dg: [make_dg_r, make_dz1],
+                       product_out1: [copy_out1], product_out0: [add_out0], warm: []}[fn]
+            tag = "dg" if fn == product_dg else "turn" if fn in (turn_dz2, turn_weight, turn_dz1) else "acc"
+            if fn == product_out0:
+                tag = ("dg", "turn")[args[1]]
+            return "bank", [(rd,) + args for rd in readers]
+
+        def run(sync_steps, tensor_steps, scalar_steps, vector_steps):
+            extra = {}
+            seen = {"bank": []}
+            depth = {"bank": 8}
+            for step in tensor_steps:
+                tag, readers = bank_use(step)
+                if len(seen[tag]) >= depth[tag]:
+                    extra[step] = seen[tag][-depth[tag]]
+                seen[tag].append(readers)
+            queues = [(sync_steps, None), (tensor_steps, None), (scalar_steps, on_scalar), (vector_steps, on_vector)]
+            at = [0, 0, 0, 0]
+            done = set()
+            while any(at[n] < len(queues[n][0]) for n in range(4)):
+                moved = False
+                for n, (steps, copy) in enumerate(queues):
+                    while at[n] < len(steps) and all(s in done for s in needs(steps[at[n]]) + extra.get(steps[at[n]], [])):
+                        step = steps[at[n]]
+                        if step[0] in (copy_dz2, copy_weight, copy_dz1, copy_out1, interleave_dz1, interleave_jh):
+                            step[0](*step[1:], copy)
+                        else:
+                            step[0](*step[1:])
+                        done.add(step)
+                        at[n] = at[n] + 1
+                        moved = True
+                assert moved, [queues[n][0][at[n]][1:] for n in range(4) if at[n] < len(queues[n][0])]
+
+        sync_steps = [(load_weight, "h", 0), (load_dz2_inputs, 0), (load_weight, "h", 1), (load_dz2_inputs, 1), (load_gate, 0, 0), (load_dz2_inputs, 2), (load_gate, 1, 0), (load_dz2_inputs, 3), (load_jh,), (load_gate, 2, 0), (load_weight, "h", 2), (load_gate, 3, 0), (load_weight, "h", 3), (load_gate, 0, 1), (load_weight, "r", 0), (load_gate, 1, 1), (load_weight, "r", 1), (load_gate, 2, 1), (load_gate, 3, 1), (load_weight, "r", 2), (load_weight, "r", 3), (store_out1, 0, 0), (store_out1, 1, 0), (store_out1, 2, 0), (store_out1, 3, 0), (store_out1, 4, 0), (store_out1, 5, 0), (store_out1, 6, 0), (store_out1, 7, 0), (store_out1, 0, 1), (store_out1, 1, 1), (store_out1, 2, 1), (store_out0, 0, 0), (store_out0, 1, 0), (store_out1, 3, 1), (store_out0, 2, 0), (store_out0, 3, 0), (store_out1, 4, 1), (store_out1, 5, 1), (store_out1, 6, 1), (store_out0, 0, 1), (store_out1, 7, 1), (store_out0, 1, 1), (store_out0, 2, 1), (store_out0, 3, 1)]
+        tensor_steps = [(turn_weight, "h", 0, 0), (turn_weight, "h", 0, 1), (turn_weight, "h", 1, 0), (turn_dz2, 0), (turn_weight, "h", 1, 1), (product_dg, 0, 0), (turn_dz2, 1), (product_dg, 1, 0), (turn_dz2, 2), (product_dg, 2, 0), (turn_dz2, 3), (turn_weight, "h", 2, 0), (turn_weight, "h", 2, 1), (product_dg, 3, 0), (turn_dz1, 0, 0), (turn_weight, "h", 3, 0), (turn_weight, "h", 3, 1), (turn_dz1, 0, 1), (product_dg, 0, 1), (turn_weight, "r", 0, 0), (turn_weight, "r", 0, 1), (product_dg, 1, 1), (product_out1, 0, 0), (product_out1, 1, 0), (product_out1, 2, 0), (product_dg, 2, 1), (product_out1, 3, 0), (product_out1, 4, 0), (product_dg, 3, 1), (product_out1, 5, 0), (product_out1, 6, 0), (product_out1, 7, 0), (turn_dz1, 1, 0), (turn_weight, "r", 1, 0), (turn_weight, "r", 1, 1), (product_out1, 0, 1), (product_out1, 1, 1), (product_out1, 2, 1), (turn_dz1, 1, 1), (turn_weight, "r", 2, 0), (product_out0, 0, 0), (product_out0, 1, 0), (turn_weight, "r", 2, 1), (turn_weight, "r", 3, 0), (product_out1, 3, 1), (product_out0, 2, 0), (turn_weight, "r", 3, 1), (product_out0, 3, 0), (product_out1, 4, 1), (product_out1, 5, 1), (product_out1, 6, 1), (product_out0, 0, 1), (product_out1, 7, 1), (product_out0, 1, 1), (product_out0, 2, 1), (product_out0, 3, 1)]
+        scalar_steps = [(square, 0), (copy_weight, "h", 1, 0), (copy_dz2, 0), (square, 1), (square, 2), (copy_dz2, 1), (square, 3), (copy_dz2, 2), (interleave_jh, 0), (interleave_jh, 1), (copy_dz2, 3), (copy_weight, "h", 2, 0), (copy_weight, "h", 2, 1), (copy_dz1, 0, 0), (copy_weight, "h", 3, 0), (copy_weight, "h", 3, 1), (interleave_jh, 2), (interleave_jh, 3), (copy_dz1, 0, 1), (copy_weight, "r", 0, 0), (copy_weight, "r", 0, 1), (copy_out1, 0, 0), (copy_out1, 1, 0), (copy_out1, 2, 0), (copy_out1, 3, 0), (copy_out1, 4, 0), (copy_out1, 5, 0), (copy_out1, 6, 0), (copy_out1, 7, 0), (copy_dz1, 1, 0), (interleave_dz1, 1, 0), (copy_weight, "r", 1, 0), (copy_weight, "r", 1, 1), (copy_out1, 0, 1), (copy_out1, 1, 1), (copy_dz1, 1, 1), (copy_out1, 2, 1), (copy_weight, "r", 2, 0), (copy_weight, "r", 2, 1), (copy_weight, "r", 3, 0), (copy_out1, 3, 1), (copy_weight, "r", 3, 1), (copy_out1, 4, 1), (copy_out1, 5, 1), (copy_out1, 6, 1), (copy_out1, 7, 1)]
+        vector_steps = [(copy_weight, "h", 0, 0), (copy_weight, "h", 0, 1), (neg_dz2, 0), (quantize_weight_part, "h", 0, 0), (quantize_weight_part, "h", 0, 1), (copy_weight, "h", 1, 1), (quantize_weight_part, "h", 1, 0), (quantize_dz2, 0), (quantize_weight_part, "h", 1, 1), (neg_dz2, 1), (gate_factor, 0, 0), (make_dg_r, 0, 0), (make_dz1, 0, 0), (quantize_dz2, 1), (neg_dz2, 2), (gate_factor, 1, 0), (make_dg_r, 1, 0), (make_dz1, 1, 0), (quantize_dz2, 2), (neg_dz2, 3), (gate_factor, 2, 0), (make_dg_r, 2, 0), (make_dz1, 2, 0), (quantize_dz2, 3), (gate_factor, 3, 0), (quantize_jh, 0), (make_dz1, 3, 0), (make_dg_r, 3, 0), (quantize_weight_part, "h", 2, 0), (quantize_weight_part, "h", 2, 1), (interleave_dz1, 0, 0), (quantize_weight_part, "h", 3, 0), (quantize_weight_part, "h", 3, 1), (interleave_dz1, 0, 1), (gate_factor, 0, 1), (quantize_dz1_tok, 0), (make_dz1, 0, 1), (make_dg_r, 0, 1), (gate_factor, 1, 1), (quantize_jh, 1), (make_dz1, 1, 1), (make_dg_r, 1, 1), (gate_factor, 2, 1), (gate_factor, 3, 1), (make_dz1, 2, 1), (make_dz1, 3, 1), (make_dg_r, 2, 1), (interleave_dz1, 1, 1), (make_dg_r, 3, 1), (quantize_dz1_feat, 0, 0), (quantize_dz1_tok, 1), (quantize_dz1_feat, 0, 1), (quantize_weight_part, "r", 0, 0), (quantize_weight_part, "r", 0, 1), (quantize_dz1_feat, 1, 0), (quantize_weight_part, "r", 1, 0), (quantize_weight_part, "r", 1, 1), (add_out0, 0, 0), (quantize_dz1_feat, 1, 1), (add_out0, 1, 0), (quantize_weight_part, "r", 2, 0), (quantize_weight_part, "r", 2, 1), (add_out0, 2, 0), (quantize_weight_part, "r", 3, 0), (add_out0, 3, 0), (quantize_weight_part, "r", 3, 1), (add_out0, 0, 1), (add_out0, 1, 1), (add_out0, 2, 1), (add_out0, 3, 1)]
+        run(sync_steps, tensor_steps, scalar_steps, vector_steps)

@@ -19,6 +19,15 @@ ACT = mybir.ActivationFunctionType
 P = 128
 PACK = 4
 HALF = 512
+QUARTER = 256
+SLOTS = range(PACK)
+HALVES = range(2)
+PASSES = range(2)
+PAIRS = range(2)
+PARTS = range(2)
+QUARTERS = range(4)
+ROW_TILES = range(H // P)
+BANKS = 8
 
 
 def tile_joint_gru_pa_v_kernel(tc, joint_h, mgn_h, W_r, W_h, U_r, U_h, b_r, b_h, r, g, y, grad_out, out_0, out_1):
@@ -28,273 +37,360 @@ def tile_joint_gru_pa_v_kernel(tc, joint_h, mgn_h, W_r, W_h, U_r, U_h, b_r, b_h,
         psum = ctx.enter_context(tc.psum_pool(name="psum", bufs=1))
         ctx.enter_context(tc.manual_schedule())
 
-        def sb(name, width, dtype, tag="", bufs=1):
-            return keep.tile([P, width], dtype, name=name, tag=tag or name, bufs=bufs, align_bytes=64)
+        def sbuf(name, width, dtype, tag=""):
+            return keep.tile([P, width], dtype, name=name, tag=tag or name, align_bytes=64)
 
-        def slots(t):
-            return t.rearrange("(p j) w -> p j w", j=PACK)
+        def mx_tiles(name, words):
+            return sbuf(name + "_codes", words, U32), sbuf(name + "_scales", words, U8)
 
-        def cols(h, width=HALF):
-            return slice(h * width, (h + 1) * width)
+        def span(n, width):
+            return slice(n * width, (n + 1) * width)
 
-        def mx_tiles(name, width):
-            return sb(name + "_codes", width, U32), sb(name + "_scales", width, U8)
+        def by_slot(tensor):
+            return tensor.rearrange("(p j) w -> p j w", j=PACK)
 
-        def quantize(dst, where, src, fmt):
-            nc.vector.quantize_mx(out=dst[0][:, where].bitcast(fmt), scales=dst[1][:, where], in_=src)
+        def quantize(operand, words, src, fmt):
+            nc.vector.quantize_mx(out=operand[0][:, words].bitcast(fmt), scales=operand[1][:, words], in_=src)
 
-        def matmul(acc, lhs, lhs_cols, lhs_fmt, rhs, rhs_cols, rhs_fmt, start, stop):
+        def matmul(acc, lhs, lhs_words, lhs_fmt, rhs, rhs_fmt, start, stop):
             nc.tensor.matmul_mx(
                 out=acc[:],
-                lhsT=lhs[0][:, lhs_cols].bitcast(lhs_fmt),
-                lhsT_scale=lhs[1][:, lhs_cols],
-                rhs=rhs[0][:, rhs_cols].bitcast(rhs_fmt),
-                rhs_scale=rhs[1][:, rhs_cols],
+                lhsT=lhs[0][:, lhs_words].bitcast(lhs_fmt),
+                lhsT_scale=lhs[1][:, lhs_words],
+                rhs=rhs[0][:].bitcast(rhs_fmt),
+                rhs_scale=rhs[1][:],
                 start=start,
                 stop=stop,
             )
 
-        ident = sb("ident", P, F32)
+        ident = sbuf("ident", P, F32)
         make_identity(nc, ident[:])
 
-        go_sb = [sb("go%d" % j, H, BF16) for j in range(PACK)]
-        y_sb = [sb("y%d" % j, H, F32) for j in range(PACK)]
-        g_sb = [sb("g%d" % j, H, F32) for j in range(PACK)]
-        r_sb = [sb("r%d" % j, H, F32) for j in range(PACK)]
-        jh_sb = sb("jh", PACK * H, BF16)
-        weights = {"h": U_h, "r": U_r}
-        u_sb = {(w, q): sb("u%s%d" % (w, q), 2 * H, BF16) for w in "hr" for q in range(4)}
+        weights = {"U_h": U_h, "U_r": U_r}
+        grad_sb = [sbuf("grad%d" % j, H, BF16) for j in SLOTS]
+        y_sb = [sbuf("y%d" % j, H, F32) for j in SLOTS]
+        g_sb = [sbuf("g%d" % j, H, F32) for j in SLOTS]
+        r_sb = [sbuf("r%d" % j, H, F32) for j in SLOTS]
+        joint_sb = sbuf("joint", PACK * H, BF16)
+        weight_sb = {(w, q): sbuf("%s_%d" % (w, q), 2 * H, BF16) for w in weights for q in QUARTERS}
 
-        dz2_mx = [mx_tiles("dz2_%d" % j, 2 * P) for j in range(PACK)]
-        u_mx = {(w, h, k): mx_tiles("u%s%d%d" % (w, h, k), HALF) for w in "hr" for h in range(2) for k in range(2)}
-        dz1_sb = [sb("dz1_%d" % h, PACK * HALF, BF16) for h in range(2)]
-        dz1_tok = [sb("dz1_tok%d" % h, PACK * HALF, BF16) for h in range(2)]
-        dz1_tok_mx = [mx_tiles("dz1_tok%d" % h, HALF) for h in range(2)]
-        dz1_feat_mx = {(h, jp): mx_tiles("dz1_feat%d%d" % (h, jp), 2 * P) for h in range(2) for jp in range(2)}
-        jh_tok = [sb("jh_tok%d" % h, PACK * HALF, BF16) for h in range(2)]
-        jh_mx = [mx_tiles("jh%d" % h, HALF) for h in range(2)]
-        u_t = {(w, h, k): sb("u_t%s%d%d" % (w, h, k), PACK * HALF, BF16) for w in "hr" for h in range(2) for k in range(2)}
-        staged = {}
+        out0_sb = [sbuf("out0_%d" % j, H, F32) for j in SLOTS]
+        dz1_sb = [sbuf("dz1_%d" % h, PACK * HALF, BF16) for h in HALVES]
+
+        dz2_feat = [sbuf("dz2_feat%d" % j, H, BF16) for j in SLOTS]
+        dz2_mx = [mx_tiles("dz2_%d" % j, 2 * P) for j in SLOTS]
+        weight_keys = [(w, h, kpass) for w in weights for h in HALVES for kpass in PASSES]
+        weight_feat = {key: sbuf("%s_feat%d%d" % key, PACK * HALF, BF16) for key in weight_keys}
+        weight_mx = {key: mx_tiles("%s_%d%d" % key, HALF) for key in weight_keys}
+        dz1_feat = {(h, pair): sbuf("dz1_feat%d%d" % (h, pair), H, BF16) for h in HALVES for pair in PAIRS}
+        dz1_feat_mx = {(h, pair): mx_tiles("dz1_feat%d%d" % (h, pair), 2 * P) for h in HALVES for pair in PAIRS}
+        dz1_tok = [sbuf("dz1_tok%d" % h, PACK * HALF, BF16) for h in HALVES]
+        dz1_tok_mx = [mx_tiles("dz1_tok%d" % h, HALF) for h in HALVES]
+        joint_tok = [sbuf("joint_tok%d" % h, PACK * HALF, BF16) for h in HALVES]
+        joint_mx = [mx_tiles("joint%d" % h, HALF) for h in HALVES]
+        gated = {}
+        filled = {}
+
 
         def load_dz2_inputs(j):
-            nc.sync.dma_start(out=y_sb[j][:], in_=slots(y)[:, j, :])
-            nc.sync.dma_start(out=go_sb[j][:], in_=slots(grad_out)[:, j, :])
-
-        def load_y(j):
-            nc.sync.dma_start(out=y_sb[j][:], in_=slots(y)[:, j, :])
+            nc.sync.dma_start(out=y_sb[j][:], in_=by_slot(y)[:, j, :])
+            nc.sync.dma_start(out=grad_sb[j][:], in_=by_slot(grad_out)[:, j, :])
 
         def load_gate(j, h):
-            nc.sync.dma_start(out=g_sb[j][:, cols(h)], in_=slots(g)[:, j, cols(h)])
-            nc.sync.dma_start(out=r_sb[j][:, cols(h)], in_=slots(r)[:, j, cols(h)])
+            nc.sync.dma_start(out=g_sb[j][:, span(h, HALF)], in_=by_slot(g)[:, j, span(h, HALF)])
+            nc.sync.dma_start(out=r_sb[j][:, span(h, HALF)], in_=by_slot(r)[:, j, span(h, HALF)])
 
         def load_weight(w, q):
-            rows = weights[w][cols(q, 2 * P), :]
-            nc.sync.dma_start(out=u_sb[w, q][:], in_=rows.rearrange("(p m) k -> p (m k)", m=2))
+            rows = weights[w][span(q, QUARTER), :]
+            nc.sync.dma_start(out=weight_sb[w, q][:], in_=rows.rearrange("(p m) k -> p (m k)", m=2))
 
-        def load_jh():
-            nc.sync.dma_start(out=jh_sb[:], in_=joint_h.rearrange("(p j) w -> p (j w)", j=PACK))
+        def load_joint():
+            nc.sync.dma_start(out=joint_sb[:], in_=joint_h.rearrange("(p j) w -> p (j w)", j=PACK))
 
-        def transpose_pair(name, src_a, src_b):
-            bank = psum.tile([P, 2, 2, P], F32, name=name, tag="bank", bufs=8)
-            for n, src in enumerate((src_a, src_b)):
-                words = src.bitcast(F32)
+        def out1_sb(t, h):
+            return (y_sb, g_sb)[h][t // 2][:, span(t % 2, HALF)]
+
+        def store_out1(t, h):
+            nc.sync.dma_start(out=out_1[span(t, P), span(h, HALF)], in_=out1_sb(t, h))
+
+        def store_out0(j):
+            nc.sync.dma_start(out=by_slot(out_0)[:, j, :], in_=out0_sb[j][:])
+
+
+        def turn(bank, sources):
+            turned = psum.tile([P, 2, 2, P], F32, name="turned", tag="bank%d" % bank)
+            for n, src in enumerate(sources):
                 for u in range(2):
-                    nc.tensor.transpose(bank[:, n, u, :], words[:, u : 2 * P : 2], ident[:])
-            return bank
+                    nc.tensor.transpose(turned[:, n, u, :], src.bitcast(F32)[:, u : 2 * P : 2], ident[:])
+            return turned
+
+        def turn_dz2(j, bank):
+            return turn(bank, [grad_sb[j][:, span(kpass, HALF)] for kpass in PASSES])
+
+        def turn_weight(w, q, kpass, bank):
+            return turn(bank, [weight_sb[w, q][:, span(2 * m + kpass, HALF)] for m in range(2)])
+
+        def turn_dz1(h, pair, bank):
+            return turn(bank, [dz1_sb[h][:, span(2 * pair + n, HALF)] for n in range(2)])
+
+        def product_dg(j, h, bank):
+            acc = psum.tile([P, HALF], F32, name="neg_dg", tag="bank%d" % bank)
+            for kpass in PASSES:
+                matmul(acc, dz2_mx[j], span(kpass, P), E5M2, weight_mx["U_h", h, kpass], E4M3, kpass == 0, kpass == 1)
+            return acc
+
+        def product_out1(t, h, bank):
+            acc = psum.tile([P, HALF], F32, name="acc1", tag="bank%d" % bank)
+            matmul(acc, joint_mx[t // 4], span(t % 4, P), E4M3, dz1_tok_mx[h], E5M2, True, True)
+            return acc
+
+        def product_out0(j, h, bank):
+            acc = psum.tile([P, HALF], F32, name="acc0", tag="bank%d" % bank)
+            for kpass in PASSES:
+                matmul(acc, dz1_feat_mx[kpass, j // 2], span(j % 2, P), E5M2, weight_mx["U_r", h, kpass], E4M3, kpass == 0, kpass == 1)
+            return acc
+
+
+        def copy_dz2(j, copy):
+            dst = dz2_feat[j][:].bitcast(F32).rearrange("p (kpass c u) -> p kpass c u", kpass=2, u=2)
+            copy(out=dst, in_=filled[turn_dz2, j][:].rearrange("p kpass u c -> p kpass c u"))
+
+        def copy_weight(w, q, kpass, copy):
+            dst = weight_feat[w, q // 2, kpass][:, span(q % 2, PACK * QUARTER)]
+            dst = dst.bitcast(F32).rearrange("p (c m u) -> p c m u", m=2, u=2)
+            copy(out=dst, in_=filled[turn_weight, w, q, kpass][:].rearrange("p m u c -> p c m u"))
+
+        def copy_dz1(h, pair, copy):
+            dst = dz1_feat[h, pair][:].bitcast(F32).rearrange("p (n c u) -> p n c u", n=2, u=2)
+            copy(out=dst, in_=filled[turn_dz1, h, pair][:].rearrange("p n u c -> p n c u"))
+
+        def copy_out1(t, h, copy):
+            copy(out=out1_sb(t, h), in_=filled[product_out1, t, h][:])
+
+        def interleave(copy, dst, src, n):
+            src = src.rearrange("p (j w) -> p j w", j=PACK)[:, :, span(n, QUARTER)]
+            copy(out=dst.rearrange("p (c i j) -> p c j i", i=4, j=PACK), in_=src.rearrange("p j (c i) -> p c j i", i=4))
+
+        def interleave_dz1(h, part, copy):
+            interleave(copy, dz1_tok[h][:, span(part, PACK * QUARTER)], dz1_sb[h][:], part)
+
+        def interleave_joint(q, copy):
+            interleave(copy, joint_tok[q // 2][:, span(q % 2, PACK * QUARTER)], joint_sb[:], q)
+
 
         def square(j):
             nc.scalar.activation(out=y_sb[j][:], in_=y_sb[j][:], func=ACT.Square)
 
         def neg_dz2(j):
-            nc.vector.scalar_tensor_tensor(out=go_sb[j][:], in0=y_sb[j][:], scalar=1.0, in1=go_sb[j][:], op0=ALU.subtract, op1=ALU.mult)
+            nc.vector.scalar_tensor_tensor(out=grad_sb[j][:], in0=y_sb[j][:], scalar=1.0, in1=grad_sb[j][:], op0=ALU.subtract, op1=ALU.mult)
 
-        def turn_dz2(j):
-            staged["dz2_bank", j] = transpose_pair("dz2_bank%d" % j, go_sb[j][:, cols(0)], go_sb[j][:, cols(1)])
+        def gate_dg(j, h):
+            gated[j, h] = sbuf("gated", HALF, F32, tag="gated%d" % j)
+            neg_dg = filled[product_dg, j, h]
+            nc.vector.scalar_tensor_tensor(out=gated[j, h][:], in0=r_sb[j][:, span(h, HALF)], scalar=1.0, in1=neg_dg[:], op0=ALU.subtract, op1=ALU.mult)
 
-        def copy_dz2(j, copy):
-            staged["dz2", j] = sb("dz2_t%d" % j, H, BF16)
-            dst = staged["dz2", j][:].bitcast(F32).rearrange("p (k c u) -> p k c u", k=2, u=2)
-            copy(out=dst, in_=staged["dz2_bank", j][:].rearrange("p k u c -> p k c u"))
-
-        def quantize_dz2(j):
-            quantize(dz2_mx[j], slice(None), staged["dz2", j][:], E5M2)
-
-        def turn_weight(w, q, k):
-            src = u_sb[w, q]
-            staged["u_bank", w, q, k] = transpose_pair("u_bank%s%d%d" % (w, q, k), src[:, cols(k)], src[:, cols(2 + k)])
-
-        def copy_weight(w, q, k, copy):
-            h, a = divmod(q, 2)
-            dst = u_t[w, h, k][:, cols(a, H)].bitcast(F32).rearrange("p (c m u) -> p c m u", m=2, u=2)
-            copy(out=dst, in_=staged["u_bank", w, q, k][:].rearrange("p m u c -> p c m u"))
-
-        def quantize_weight(w, h, k):
-            quantize(u_mx[w, h, k], slice(None), u_t[w, h, k][:], E4M3)
-
-        def quantize_weight_part(w, q, k):
-            h, a = divmod(q, 2)
-            quantize(u_mx[w, h, k], cols(a, 2 * P), u_t[w, h, k][:, cols(a, H)], E4M3)
-
-        def product_dg(j, h):
-            staged["dg", j, h] = psum.tile([P, HALF], F32, name="dg%d%d" % (j, h), tag="bank", bufs=8)
-            for k in range(2):
-                matmul(staged["dg", j, h], dz2_mx[j], cols(k, P), E5M2, u_mx["h", h, k], slice(None), E4M3, k == 0, k == 1)
-
-        def gate_factor(j, h):
-            nc.vector.scalar_tensor_tensor(out=g_sb[j][:, cols(h)], in0=r_sb[j][:, cols(h)], scalar=1.0, in1=g_sb[j][:, cols(h)], op0=ALU.subtract, op1=ALU.mult)
+        def dg_times_r(j, h):
+            neg_dg = filled[product_dg, j, h]
+            nc.vector.scalar_tensor_tensor(out=out0_sb[j][:, span(h, HALF)], in0=neg_dg[:], scalar=-1.0, in1=r_sb[j][:, span(h, HALF)], op0=ALU.mult, op1=ALU.mult)
 
         def make_dz1(j, h):
-            nc.vector.tensor_tensor(out=dz1_sb[h][:, cols(j)], in0=staged["dg", j, h][:], in1=g_sb[j][:, cols(h)], op=ALU.mult)
-
-        def make_dg_r(j, h):
-            nc.vector.scalar_tensor_tensor(out=r_sb[j][:, cols(h)], in0=staged["dg", j, h][:], scalar=-1.0, in1=r_sb[j][:, cols(h)], op0=ALU.mult, op1=ALU.mult)
-
-        def interleave(copy, dst, src):
-            copy(out=dst.rearrange("p (c i j) -> p c j i", i=4, j=PACK), in_=src.rearrange("p j (c i) -> p c j i", i=4))
-
-        def interleave_dz1(h, part, copy):
-            src = dz1_sb[h][:].rearrange("p (j c) -> p j c", j=PACK)[:, :, cols(part, 2 * P)]
-            interleave(copy, dz1_tok[h][:, cols(part, H)], src)
-
-        def quantize_dz1_tok(h):
-            quantize(dz1_tok_mx[h], slice(None), dz1_tok[h][:], E5M2)
-
-        def interleave_jh(q, copy):
-            src = jh_sb[:].rearrange("p (j c) -> p j c", j=PACK)[:, :, cols(q, 2 * P)]
-            interleave(copy, jh_tok[q // 2][:, cols(q % 2, H)], src)
-
-        def quantize_jh(h):
-            quantize(jh_mx[h], slice(None), jh_tok[h][:], E4M3)
-
-        def turn_dz1(h, jp):
-            staged["dz1_bank", h, jp] = transpose_pair("dz1_bank%d%d" % (h, jp), dz1_sb[h][:, cols(2 * jp)], dz1_sb[h][:, cols(2 * jp + 1)])
-
-        def copy_dz1(h, jp, copy):
-            staged["dz1", h, jp] = sb("dz1_t%d%d" % (h, jp), H, BF16)
-            dst = staged["dz1", h, jp][:].bitcast(F32).rearrange("p (n c u) -> p n c u", n=2, u=2)
-            copy(out=dst, in_=staged["dz1_bank", h, jp][:].rearrange("p n u c -> p n c u"))
-
-        def quantize_dz1_feat(h, jp):
-            quantize(dz1_feat_mx[h, jp], slice(None), staged["dz1", h, jp][:], E5M2)
-
-        def product_out1(t, h):
-            staged["acc1", t, h] = psum.tile([P, HALF], F32, name="acc1_%d%d" % (t, h), tag="bank", bufs=8)
-            matmul(staged["acc1", t, h], jh_mx[t // 4], cols(t % 4, P), E4M3, dz1_tok_mx[h], slice(None), E5M2, True, True)
-
-        def out1_stage(t, h):
-            return (y_sb, g_sb)[h][t // 2][:, cols(t % 2)]
-
-        def copy_out1(t, h, copy):
-            copy(out=out1_stage(t, h), in_=staged["acc1", t, h][:])
-
-        def store_out1(t, h):
-            nc.sync.dma_start(out=out_1[cols(t, P), cols(h)], in_=out1_stage(t, h))
-
-        def product_out0(j, h):
-            staged["acc0", j, h] = psum.tile([P, HALF], F32, name="acc0_%d%d" % (j, h), tag="bank", bufs=8)
-            for k in range(2):
-                matmul(staged["acc0", j, h], dz1_feat_mx[k, j // 2], cols(j % 2, P), E5M2, u_mx["r", h, k], slice(None), E4M3, k == 0, k == 1)
+            engine = nc.vector if j == SLOTS[-1] else nc.gpsimd
+            engine.tensor_tensor(out=dz1_sb[h][:, span(j, HALF)], in0=gated[j, h][:], in1=g_sb[j][:, span(h, HALF)], op=ALU.mult)
 
         def add_out0(j, h):
-            nc.vector.tensor_tensor(out=r_sb[j][:, cols(h)], in0=staged["acc0", j, h][:], in1=r_sb[j][:, cols(h)], op=ALU.add)
+            dst = out0_sb[j][:, span(h, HALF)]
+            nc.vector.tensor_tensor(out=dst, in0=filled[product_out0, j, h][:], in1=dst, op=ALU.add)
 
-        def store_out0(j, h):
-            nc.sync.dma_start(out=slots(out_0)[:, j, cols(h)], in_=r_sb[j][:, cols(h)])
+        def quantize_dz2(j):
+            quantize(dz2_mx[j], slice(None), dz2_feat[j][:], E5M2)
 
-        def warm(n, place):
-            bank = psum.tile([P, P], F32, name="warm", tag="bank", bufs=8)
-            for i in range(n):
-                nc.tensor.matmul(bank[:], ident[:], ident[:], start=True, stop=True)
+        def quantize_weight(w, q, kpass):
+            key = (w, q // 2, kpass)
+            quantize(weight_mx[key], span(q % 2, QUARTER), weight_feat[key][:, span(q % 2, PACK * QUARTER)], E4M3)
 
-        on_scalar = nc.scalar.copy
-        on_vector = nc.vector.tensor_copy
+        def quantize_dz1_feat(h, pair):
+            quantize(dz1_feat_mx[h, pair], slice(None), dz1_feat[h, pair][:], E5M2)
 
-        def needs(step):
-            fn, args = step[0], step[1:]
-            if fn == neg_dz2:
-                return [(square,) + args]
-            if fn == turn_dz2:
-                return [(neg_dz2,) + args]
-            if fn == copy_dz2:
-                return [(turn_dz2,) + args]
-            if fn == quantize_dz2:
-                return [(copy_dz2,) + args]
-            if fn == copy_weight:
-                return [(turn_weight,) + args]
-            if fn == quantize_weight_part:
-                return [(copy_weight,) + args]
-            if fn == quantize_weight:
-                w, h, k = args
-                return [(copy_weight, w, 2 * h, k), (copy_weight, w, 2 * h + 1, k)]
-            if fn == product_dg:
-                j, h = args
-                return [(quantize_dz2, j)] + [(quantize_weight_part, "h", 2 * h + a, k) for a in range(2) for k in range(2)]
-            if fn == make_dg_r or fn == make_dz1:
-                return [(product_dg,) + args, (gate_factor,) + args]
-            if fn == interleave_dz1:
-                return [(make_dz1, j, args[0]) for j in range(PACK)]
-            if fn == quantize_dz1_tok:
-                return [(interleave_dz1, args[0], part) for part in range(2)]
-            if fn == quantize_jh:
-                return [(interleave_jh, 2 * args[0] + part) for part in range(2)]
-            if fn == turn_dz1:
-                return [(make_dz1, 2 * args[1] + n, args[0]) for n in range(2)]
-            if fn == copy_dz1:
-                return [(turn_dz1,) + args]
-            if fn == quantize_dz1_feat:
-                return [(copy_dz1,) + args]
-            if fn == product_out1:
-                return [(quantize_jh, args[0] // 4), (quantize_dz1_tok, args[1])]
-            if fn == copy_out1:
-                return [(product_out1,) + args]
-            if fn == store_out1:
-                return [(copy_out1,) + args]
-            if fn == product_out0:
-                j, h = args
-                return [(quantize_dz1_feat, k, j // 2) for k in range(2)] + [(quantize_weight_part, "r", 2 * h + a, k) for a in range(2) for k in range(2)]
-            if fn == add_out0:
-                return [(product_out0,) + args]
-            if fn == store_out0:
-                return [(add_out0,) + args]
-            return []
+        def quantize_dz1_tok(h, part):
+            quantize(dz1_tok_mx[h], span(part, QUARTER), dz1_tok[h][:, span(part, PACK * QUARTER)], E5M2)
 
-        def bank_use(step):
-            fn, args = step[0], step[1:]
-            readers = {turn_dz2: [copy_dz2], turn_weight: [copy_weight], turn_dz1: [copy_dz1], product_dg: [make_dg_r, make_dz1],
-                       product_out1: [copy_out1], product_out0: [add_out0], warm: []}[fn]
-            tag = "dg" if fn == product_dg else "turn" if fn in (turn_dz2, turn_weight, turn_dz1) else "acc"
-            if fn == product_out0:
-                tag = ("dg", "turn")[args[1]]
-            return "bank", [(rd,) + args for rd in readers]
+        def quantize_joint(h):
+            quantize(joint_mx[h], slice(None), joint_tok[h][:], E4M3)
 
-        def run(sync_steps, tensor_steps, scalar_steps, vector_steps):
-            extra = {}
-            seen = {"bank": []}
-            depth = {"bank": 8}
-            for step in tensor_steps:
-                tag, readers = bank_use(step)
-                if len(seen[tag]) >= depth[tag]:
-                    extra[step] = seen[tag][-depth[tag]]
-                seen[tag].append(readers)
-            queues = [(sync_steps, None), (tensor_steps, None), (scalar_steps, on_scalar), (vector_steps, on_vector)]
-            at = [0, 0, 0, 0]
-            done = set()
-            while any(at[n] < len(queues[n][0]) for n in range(4)):
-                moved = False
-                for n, (steps, copy) in enumerate(queues):
-                    while at[n] < len(steps) and all(s in done for s in needs(steps[at[n]]) + extra.get(steps[at[n]], [])):
-                        step = steps[at[n]]
-                        if step[0] in (copy_dz2, copy_weight, copy_dz1, copy_out1, interleave_dz1, interleave_jh):
-                            step[0](*step[1:], copy)
-                        else:
-                            step[0](*step[1:])
-                        done.add(step)
-                        at[n] = at[n] + 1
-                        moved = True
-                assert moved, [queues[n][0][at[n]][1:] for n in range(4) if at[n] < len(queues[n][0])]
 
-        sync_steps = [(load_weight, "h", 0), (load_dz2_inputs, 0), (load_weight, "h", 1), (load_dz2_inputs, 1), (load_gate, 0, 0), (load_dz2_inputs, 2), (load_gate, 1, 0), (load_dz2_inputs, 3), (load_jh,), (load_gate, 2, 0), (load_weight, "h", 2), (load_gate, 3, 0), (load_weight, "h", 3), (load_gate, 0, 1), (load_weight, "r", 0), (load_gate, 1, 1), (load_weight, "r", 1), (load_gate, 2, 1), (load_gate, 3, 1), (load_weight, "r", 2), (load_weight, "r", 3), (store_out1, 0, 0), (store_out1, 1, 0), (store_out1, 2, 0), (store_out1, 3, 0), (store_out1, 4, 0), (store_out1, 5, 0), (store_out1, 6, 0), (store_out1, 7, 0), (store_out1, 0, 1), (store_out1, 1, 1), (store_out1, 2, 1), (store_out0, 0, 0), (store_out0, 1, 0), (store_out1, 3, 1), (store_out0, 2, 0), (store_out0, 3, 0), (store_out1, 4, 1), (store_out1, 5, 1), (store_out1, 6, 1), (store_out0, 0, 1), (store_out1, 7, 1), (store_out0, 1, 1), (store_out0, 2, 1), (store_out0, 3, 1)]
-        tensor_steps = [(turn_weight, "h", 0, 0), (turn_weight, "h", 0, 1), (turn_weight, "h", 1, 0), (turn_dz2, 0), (turn_weight, "h", 1, 1), (product_dg, 0, 0), (turn_dz2, 1), (product_dg, 1, 0), (turn_dz2, 2), (product_dg, 2, 0), (turn_dz2, 3), (turn_weight, "h", 2, 0), (turn_weight, "h", 2, 1), (product_dg, 3, 0), (turn_dz1, 0, 0), (turn_weight, "h", 3, 0), (turn_weight, "h", 3, 1), (turn_dz1, 0, 1), (product_dg, 0, 1), (turn_weight, "r", 0, 0), (turn_weight, "r", 0, 1), (product_dg, 1, 1), (product_out1, 0, 0), (product_out1, 1, 0), (product_out1, 2, 0), (product_dg, 2, 1), (product_out1, 3, 0), (product_out1, 4, 0), (product_dg, 3, 1), (product_out1, 5, 0), (product_out1, 6, 0), (product_out1, 7, 0), (turn_dz1, 1, 0), (turn_weight, "r", 1, 0), (turn_weight, "r", 1, 1), (product_out1, 0, 1), (product_out1, 1, 1), (product_out1, 2, 1), (turn_dz1, 1, 1), (turn_weight, "r", 2, 0), (product_out0, 0, 0), (product_out0, 1, 0), (turn_weight, "r", 2, 1), (turn_weight, "r", 3, 0), (product_out1, 3, 1), (product_out0, 2, 0), (turn_weight, "r", 3, 1), (product_out0, 3, 0), (product_out1, 4, 1), (product_out1, 5, 1), (product_out1, 6, 1), (product_out0, 0, 1), (product_out1, 7, 1), (product_out0, 1, 1), (product_out0, 2, 1), (product_out0, 3, 1)]
-        scalar_steps = [(square, 0), (copy_weight, "h", 1, 0), (copy_dz2, 0), (square, 1), (square, 2), (copy_dz2, 1), (square, 3), (copy_dz2, 2), (interleave_jh, 0), (interleave_jh, 1), (copy_dz2, 3), (copy_weight, "h", 2, 0), (copy_weight, "h", 2, 1), (copy_dz1, 0, 0), (copy_weight, "h", 3, 0), (copy_weight, "h", 3, 1), (interleave_jh, 2), (interleave_jh, 3), (copy_dz1, 0, 1), (copy_weight, "r", 0, 0), (copy_weight, "r", 0, 1), (copy_out1, 0, 0), (copy_out1, 1, 0), (copy_out1, 2, 0), (copy_out1, 3, 0), (copy_out1, 4, 0), (copy_out1, 5, 0), (copy_out1, 6, 0), (copy_out1, 7, 0), (copy_dz1, 1, 0), (interleave_dz1, 1, 0), (copy_weight, "r", 1, 0), (copy_weight, "r", 1, 1), (copy_out1, 0, 1), (copy_out1, 1, 1), (copy_dz1, 1, 1), (copy_out1, 2, 1), (copy_weight, "r", 2, 0), (copy_weight, "r", 2, 1), (copy_weight, "r", 3, 0), (copy_out1, 3, 1), (copy_weight, "r", 3, 1), (copy_out1, 4, 1), (copy_out1, 5, 1), (copy_out1, 6, 1), (copy_out1, 7, 1)]
-        vector_steps = [(copy_weight, "h", 0, 0), (copy_weight, "h", 0, 1), (neg_dz2, 0), (quantize_weight_part, "h", 0, 0), (quantize_weight_part, "h", 0, 1), (copy_weight, "h", 1, 1), (quantize_weight_part, "h", 1, 0), (quantize_dz2, 0), (quantize_weight_part, "h", 1, 1), (neg_dz2, 1), (gate_factor, 0, 0), (make_dg_r, 0, 0), (make_dz1, 0, 0), (quantize_dz2, 1), (neg_dz2, 2), (gate_factor, 1, 0), (make_dg_r, 1, 0), (make_dz1, 1, 0), (quantize_dz2, 2), (neg_dz2, 3), (gate_factor, 2, 0), (make_dg_r, 2, 0), (make_dz1, 2, 0), (quantize_dz2, 3), (gate_factor, 3, 0), (quantize_jh, 0), (make_dz1, 3, 0), (make_dg_r, 3, 0), (quantize_weight_part, "h", 2, 0), (quantize_weight_part, "h", 2, 1), (interleave_dz1, 0, 0), (quantize_weight_part, "h", 3, 0), (quantize_weight_part, "h", 3, 1), (interleave_dz1, 0, 1), (gate_factor, 0, 1), (quantize_dz1_tok, 0), (make_dz1, 0, 1), (make_dg_r, 0, 1), (gate_factor, 1, 1), (quantize_jh, 1), (make_dz1, 1, 1), (make_dg_r, 1, 1), (gate_factor, 2, 1), (gate_factor, 3, 1), (make_dz1, 2, 1), (make_dz1, 3, 1), (make_dg_r, 2, 1), (interleave_dz1, 1, 1), (make_dg_r, 3, 1), (quantize_dz1_feat, 0, 0), (quantize_dz1_tok, 1), (quantize_dz1_feat, 0, 1), (quantize_weight_part, "r", 0, 0), (quantize_weight_part, "r", 0, 1), (quantize_dz1_feat, 1, 0), (quantize_weight_part, "r", 1, 0), (quantize_weight_part, "r", 1, 1), (add_out0, 0, 0), (quantize_dz1_feat, 1, 1), (add_out0, 1, 0), (quantize_weight_part, "r", 2, 0), (quantize_weight_part, "r", 2, 1), (add_out0, 2, 0), (quantize_weight_part, "r", 3, 0), (add_out0, 3, 0), (quantize_weight_part, "r", 3, 1), (add_out0, 0, 1), (add_out0, 1, 1), (add_out0, 2, 1), (add_out0, 3, 1)]
-        run(sync_steps, tensor_steps, scalar_steps, vector_steps)
+        def each(fn, *ranges):
+            steps = [(fn,)]
+            for values in ranges:
+                steps = [step + (value,) for step in steps for value in values]
+            return steps
+
+        def by_half(fn, first, h):
+            return each(fn, first, [h])
+
+        def weight_steps(fn, w, quarters):
+            return each(fn, [w], quarters, PASSES)
+
+        sync_steps = (
+            [(load_weight, "U_h", 0), (load_dz2_inputs, 0), (load_weight, "U_h", 1)]
+            + each(load_dz2_inputs, SLOTS[1:])
+            + each(load_weight, ["U_h"], [2, 3])
+            + by_half(load_gate, SLOTS, 0)
+            + [(load_joint,)]
+            + each(load_weight, ["U_r"], [0, 1])
+            + by_half(load_gate, SLOTS, 1)
+            + each(load_weight, ["U_r"], [2, 3])
+            + by_half(store_out1, ROW_TILES, 0)
+            + by_half(store_out1, ROW_TILES, 1)
+            + each(store_out0, SLOTS)
+        )
+
+        tensor_steps = (
+            weight_steps(turn_weight, "U_h", [0, 1])
+            + each(turn_dz2, [0, 1])
+            + [(product_dg, 0, 0), (turn_dz2, 2), (turn_weight, "U_h", 2, 0), (turn_dz2, 3), (turn_weight, "U_h", 2, 1)]
+            + by_half(product_dg, SLOTS[1:], 0)
+            + weight_steps(turn_weight, "U_h", [3])
+            + each(turn_dz1, [0], PAIRS)
+            + by_half(product_dg, SLOTS, 1)
+            + weight_steps(turn_weight, "U_r", [0])
+            + by_half(product_out1, ROW_TILES[:2], 0)
+            + weight_steps(turn_weight, "U_r", [1])
+            + by_half(product_out1, ROW_TILES[2:], 0)
+            + [(turn_dz1, 1, 0)]
+            + weight_steps(turn_weight, "U_r", [2, 3])
+            + [(turn_dz1, 1, 1)]
+            + by_half(product_out1, ROW_TILES, 1)
+            + each(product_out0, SLOTS, HALVES)
+        )
+
+        scalar_steps = (
+            [(square, 0), (square, 1), (copy_dz2, 0), (square, 2), (square, 3), (copy_dz2, 1), (copy_dz2, 2)]
+            + [(copy_weight, "U_h", 2, 0), (copy_dz2, 3), (copy_weight, "U_h", 2, 1)]
+            + weight_steps(copy_weight, "U_h", [3])
+            + [(copy_dz1, 0, 0)]
+            + each(interleave_joint, QUARTERS[:-1])
+            + [(copy_dz1, 0, 1)]
+            + weight_steps(copy_weight, "U_r", [0])
+            + by_half(copy_out1, ROW_TILES[:2], 0)
+            + weight_steps(copy_weight, "U_r", [1])
+            + by_half(copy_out1, ROW_TILES[2:], 0)
+            + weight_steps(copy_weight, "U_r", [2])
+            + by_half(copy_out1, ROW_TILES, 1)
+        )
+
+        def read_dg(h):
+            return [(fn, j, h) for j in SLOTS for fn in (gate_dg, dg_times_r)] + [(make_dz1, SLOTS[-1], h)]
+
+        vector_steps = (
+            weight_steps(copy_weight, "U_h", [0])
+            + [(neg_dz2, 0)]
+            + weight_steps(quantize_weight, "U_h", [0])
+            + weight_steps(copy_weight, "U_h", [1])
+            + [(neg_dz2, 1)]
+            + weight_steps(quantize_weight, "U_h", [1])
+            + [(quantize_dz2, 0), (neg_dz2, 2), (neg_dz2, 3), (quantize_dz2, 1), (quantize_dz2, 2)]
+            + [(quantize_weight, "U_h", 2, 0), (quantize_dz2, 3)]
+            + read_dg(0)
+            + [(quantize_weight, "U_h", 2, 1)]
+            + weight_steps(quantize_weight, "U_h", [3])
+            + each(interleave_dz1, [0], PARTS)
+            + [(interleave_joint, QUARTERS[-1])]
+            + each(quantize_dz1_tok, [0], PARTS)
+            + [(quantize_joint, 0), (quantize_dz1_feat, 0, 0), (quantize_joint, 1)]
+            + read_dg(1)
+            + [(quantize_dz1_feat, 0, 1)]
+            + each(interleave_dz1, [1], PARTS)
+            + each(quantize_dz1_tok, [1], PARTS)
+            + each(copy_dz1, [1], PAIRS)
+            + weight_steps(copy_weight, "U_r", [3])
+            + weight_steps(quantize_weight, "U_r", [0, 1])
+            + each(quantize_dz1_feat, [1], PAIRS)
+            + weight_steps(quantize_weight, "U_r", [2, 3])
+            + each(add_out0, SLOTS, HALVES)
+        )
+
+        gpsimd_steps = by_half(make_dz1, SLOTS[:-1], 0) + by_half(make_dz1, SLOTS[:-1], 1)
+
+        all_banks_from = tensor_steps.index((product_out1, 6, 0))
+        early = [step for step in tensor_steps[:all_banks_from] if step[0] != product_dg]
+        bank_of = dict(
+            [(step, step[1]) for step in tensor_steps if step[0] == product_dg]
+            + [(step, PACK + n % (BANKS - PACK)) for n, step in enumerate(early)]
+            + [(step, n % BANKS) for n, step in enumerate(tensor_steps[all_banks_from:])]
+        )
+
+
+        def weight_half(w, h):
+            return weight_steps(quantize_weight, w, [2 * h, 2 * h + 1])
+
+        reads = {
+            square: lambda j: [(load_dz2_inputs, j)],
+            neg_dz2: lambda j: [(square, j)],
+            turn_dz2: lambda j: [(neg_dz2, j)],
+            copy_dz2: lambda j: [(turn_dz2, j)],
+            quantize_dz2: lambda j: [(copy_dz2, j)],
+            turn_weight: lambda w, q, kpass: [(load_weight, w, q)],
+            copy_weight: lambda w, q, kpass: [(turn_weight, w, q, kpass)],
+            quantize_weight: lambda w, q, kpass: [(copy_weight, w, q, kpass)],
+            product_dg: lambda j, h: [(quantize_dz2, j)] + weight_half("U_h", h),
+            gate_dg: lambda j, h: [(load_gate, j, h), (product_dg, j, h)] + each(make_dz1, [j], HALVES[:h]),
+            dg_times_r: lambda j, h: [(load_gate, j, h), (product_dg, j, h)],
+            make_dz1: lambda j, h: [(gate_dg, j, h)],
+            turn_dz1: lambda h, pair: by_half(make_dz1, [2 * pair, 2 * pair + 1], h),
+            copy_dz1: lambda h, pair: [(turn_dz1, h, pair)],
+            quantize_dz1_feat: lambda h, pair: [(copy_dz1, h, pair)],
+            interleave_dz1: lambda h, part: by_half(make_dz1, SLOTS, h),
+            quantize_dz1_tok: lambda h, part: [(interleave_dz1, h, part)],
+            interleave_joint: lambda q: [(load_joint,)],
+            quantize_joint: lambda h: each(interleave_joint, [2 * h, 2 * h + 1]),
+            product_out1: lambda t, h: [(quantize_joint, t // 4)] + each(quantize_dz1_tok, [h], PARTS),
+            copy_out1: lambda t, h: [(product_out1, t, h)],
+            store_out1: lambda t, h: [(copy_out1, t, h)],
+            product_out0: lambda j, h: each(quantize_dz1_feat, PASSES, [j // 2]) + weight_half("U_r", h),
+            add_out0: lambda j, h: [(product_out0, j, h), (dg_times_r, j, h)],
+            store_out0: lambda j: each(add_out0, [j], HALVES),
+        }
+        last_reader = {
+            turn_dz2: copy_dz2,
+            turn_weight: copy_weight,
+            turn_dz1: copy_dz1,
+            product_dg: dg_times_r,
+            product_out1: copy_out1,
+            product_out0: add_out0,
+        }
+        copies = (copy_dz2, copy_weight, copy_dz1, copy_out1, interleave_dz1, interleave_joint)
+
+        waits_for = {}
+        bank_freed_by = {}
+        for step in tensor_steps:
+            waits_for[step] = bank_freed_by.get(bank_of[step], [])
+            bank_freed_by[bank_of[step]] = [(last_reader[step[0]],) + step[1:]]
+
+        def ready(step):
+            sources = reads[step[0]](*step[1:]) if step[0] in reads else []
+            return all(source in written for source in sources + waits_for.get(step, []))
+
+        queues = [
+            (sync_steps, None),
+            (tensor_steps, None),
+            (scalar_steps, nc.scalar.copy),
+            (vector_steps, nc.vector.tensor_copy),
+            (gpsimd_steps, None),
+        ]
+        written = set()
+        while len(written) < sum(len(steps) for steps, copy in queues):
+            before = len(written)
+            for steps, copy in queues:
+                for step in steps:
+                    if step in written:
+                        continue
+                    if not ready(step):
+                        break
+                    if step in bank_of:
+                        filled[step] = step[0](*step[1:], bank_of[step])
+                    elif step[0] in copies:
+                        step[0](*step[1:], copy)
+                    else:
+                        step[0](*step[1:])
+                    written.add(step)
+            assert len(written) > before, "the queues wait for each other"

@@ -67,12 +67,12 @@ def tile_joint_gru_pa_v_kernel(tc, joint_h, mgn_h, W_r, W_h, U_r, U_h, b_r, b_h,
         make_identity(nc, ident[:])
 
         weights = {"U_h": U_h, "U_r": U_r}
-        grad_sb = [sbuf("grad%d" % j, H, BF16) for j in SLOTS]
-        y_sb = [sbuf("y%d" % j, H, F32) for j in SLOTS]
-        g_sb = [sbuf("g%d" % j, H, F32) for j in SLOTS]
-        r_sb = [sbuf("r%d" % j, H, F32) for j in SLOTS]
+        grad_sb = sbuf("grad", PACK * H, BF16)
+        y_sb = sbuf("y", PACK * H, F32)
+        g_sb = [sbuf("g%d" % h, PACK * HALF, F32) for h in HALVES]
+        r_sb = [sbuf("r%d" % h, PACK * HALF, F32) for h in HALVES]
         joint_sb = sbuf("joint", PACK * H, BF16)
-        weight_sb = {(w, q): sbuf("%s_%d" % (w, q), 2 * H, BF16) for w in weights for q in QUARTERS}
+        weight_sb = {(w, h): sbuf("%s_%d" % (w, h), PACK * H, BF16) for w in weights for h in HALVES}
 
         out0_sb = [sbuf("out0_%d" % j, H, F32) for j in SLOTS]
         dz1_sb = [sbuf("dz1_%d" % h, PACK * HALF, BF16) for h in HALVES]
@@ -92,26 +92,32 @@ def tile_joint_gru_pa_v_kernel(tc, joint_h, mgn_h, W_r, W_h, U_r, U_h, b_r, b_h,
         filled = {}
 
 
-        def load_dz2_inputs(j):
-            nc.sync.dma_start(out=y_sb[j][:], in_=by_slot(y)[:, j, :])
-            nc.sync.dma_start(out=grad_sb[j][:], in_=by_slot(grad_out)[:, j, :])
+        def load_y(j):
+            nc.sync.dma_start(out=y_sb[:, span(j, H)], in_=by_slot(y)[:, j, :])
 
-        def load_gate(j, h):
-            nc.sync.dma_start(out=g_sb[j][:, span(h, HALF)], in_=by_slot(g)[:, j, span(h, HALF)])
-            nc.sync.dma_start(out=r_sb[j][:, span(h, HALF)], in_=by_slot(r)[:, j, span(h, HALF)])
+        def load_grad(pair):
+            dst = grad_sb[:, span(pair, 2 * H)].rearrange("p (j w) -> p j w", j=2)
+            nc.sync.dma_start(out=dst, in_=by_slot(grad_out)[:, span(pair, 2), :])
 
-        def load_weight(w, q):
-            rows = weights[w][span(q, QUARTER), :]
-            nc.sync.dma_start(out=weight_sb[w, q][:], in_=rows.rearrange("(p m) k -> p (m k)", m=2))
+        def load_gate(pair, h):
+            for dst, src in ((r_sb, r), (g_sb, g)):
+                dst = dst[h][:, span(pair, 2 * HALF)].rearrange("p (j w) -> p j w", j=2)
+                nc.sync.dma_start(out=dst, in_=by_slot(src)[:, span(pair, 2), span(h, HALF)])
+
+        def load_weight(w, h):
+            rows = weights[w][span(h, HALF), :]
+            nc.sync.dma_start(out=weight_sb[w, h][:], in_=rows.rearrange("(p m) k -> p (m k)", m=PACK))
 
         def load_joint():
             nc.sync.dma_start(out=joint_sb[:], in_=joint_h.rearrange("(p j) w -> p (j w)", j=PACK))
 
-        def out1_sb(t, h):
-            return (y_sb, g_sb)[h][t // 2][:, span(t % 2, HALF)]
+        def out1_sb(t, h, tiles):
+            stage, first = (y_sb, t) if h == 0 else (g_sb[t // PACK], t % PACK)
+            return stage[:, first * HALF : (first + tiles) * HALF]
 
         def store_out1(t, h):
-            nc.sync.dma_start(out=out_1[span(t, P), span(h, HALF)], in_=out1_sb(t, h))
+            dst = out_1[t * P : (t + 2) * P, span(h, HALF)].rearrange("(n p) w -> p n w", p=P)
+            nc.sync.dma_start(out=dst, in_=out1_sb(t, h, 2).rearrange("p (n w) -> p n w", n=2))
 
         def store_out0(j):
             nc.sync.dma_start(out=by_slot(out_0)[:, j, :], in_=out0_sb[j][:])
@@ -125,10 +131,10 @@ def tile_joint_gru_pa_v_kernel(tc, joint_h, mgn_h, W_r, W_h, U_r, U_h, b_r, b_h,
             return turned
 
         def turn_dz2(j, bank):
-            return turn(bank, [grad_sb[j][:, span(kpass, HALF)] for kpass in PASSES])
+            return turn(bank, [grad_sb[:, span(2 * j + kpass, HALF)] for kpass in PASSES])
 
-        def turn_weight(w, q, kpass, bank):
-            return turn(bank, [weight_sb[w, q][:, span(2 * m + kpass, HALF)] for m in range(2)])
+        def turn_weight(w, h, kpass, pair, bank):
+            return turn(bank, [weight_sb[w, h][:, span(2 * m + kpass, HALF)] for m in (2 * pair, 2 * pair + 1)])
 
         def turn_dz1(h, pair, bank):
             return turn(bank, [dz1_sb[h][:, span(2 * pair + n, HALF)] for n in range(2)])
@@ -155,17 +161,16 @@ def tile_joint_gru_pa_v_kernel(tc, joint_h, mgn_h, W_r, W_h, U_r, U_h, b_r, b_h,
             dst = dz2_feat[j][:].bitcast(F32).rearrange("p (kpass c u) -> p kpass c u", kpass=2, u=2)
             copy(out=dst, in_=filled[turn_dz2, j][:].rearrange("p kpass u c -> p kpass c u"))
 
-        def copy_weight(w, q, kpass, copy):
-            dst = weight_feat[w, q // 2, kpass][:, span(q % 2, PACK * QUARTER)]
-            dst = dst.bitcast(F32).rearrange("p (c m u) -> p c m u", m=2, u=2)
-            copy(out=dst, in_=filled[turn_weight, w, q, kpass][:].rearrange("p m u c -> p c m u"))
+        def copy_weight(w, h, kpass, pair, copy):
+            dst = weight_feat[w, h, kpass][:].bitcast(F32).rearrange("p (c pair n u) -> p pair c n u", pair=2, n=2, u=2)
+            copy(out=dst[:, pair], in_=filled[turn_weight, w, h, kpass, pair][:].rearrange("p n u c -> p c n u"))
 
         def copy_dz1(h, pair, copy):
             dst = dz1_feat[h, pair][:].bitcast(F32).rearrange("p (n c u) -> p n c u", n=2, u=2)
             copy(out=dst, in_=filled[turn_dz1, h, pair][:].rearrange("p n u c -> p n c u"))
 
         def copy_out1(t, h, copy):
-            copy(out=out1_sb(t, h), in_=filled[product_out1, t, h][:])
+            copy(out=out1_sb(t, h, 1), in_=filled[product_out1, t, h][:])
 
         def interleave(copy, dst, src, n):
             src = src.rearrange("p (j w) -> p j w", j=PACK)[:, :, span(n, QUARTER)]
@@ -179,23 +184,24 @@ def tile_joint_gru_pa_v_kernel(tc, joint_h, mgn_h, W_r, W_h, U_r, U_h, b_r, b_h,
 
 
         def square(j):
-            nc.scalar.activation(out=y_sb[j][:], in_=y_sb[j][:], func=ACT.Square)
+            nc.scalar.activation(out=y_sb[:, span(j, H)], in_=y_sb[:, span(j, H)], func=ACT.Square)
 
         def neg_dz2(j):
-            nc.vector.scalar_tensor_tensor(out=grad_sb[j][:], in0=y_sb[j][:], scalar=1.0, in1=grad_sb[j][:], op0=ALU.subtract, op1=ALU.mult)
+            grad = grad_sb[:, span(j, H)]
+            nc.vector.scalar_tensor_tensor(out=grad, in0=y_sb[:, span(j, H)], scalar=1.0, in1=grad, op0=ALU.subtract, op1=ALU.mult)
 
         def gate_dg(j, h):
             gated[j, h] = sbuf("gated", HALF, F32, tag="gated%d" % j)
             neg_dg = filled[product_dg, j, h]
-            nc.vector.scalar_tensor_tensor(out=gated[j, h][:], in0=r_sb[j][:, span(h, HALF)], scalar=1.0, in1=neg_dg[:], op0=ALU.subtract, op1=ALU.mult)
+            nc.vector.scalar_tensor_tensor(out=gated[j, h][:], in0=r_sb[h][:, span(j, HALF)], scalar=1.0, in1=neg_dg[:], op0=ALU.subtract, op1=ALU.mult)
 
         def dg_times_r(j, h):
             neg_dg = filled[product_dg, j, h]
-            nc.vector.scalar_tensor_tensor(out=out0_sb[j][:, span(h, HALF)], in0=neg_dg[:], scalar=-1.0, in1=r_sb[j][:, span(h, HALF)], op0=ALU.mult, op1=ALU.mult)
+            nc.vector.scalar_tensor_tensor(out=out0_sb[j][:, span(h, HALF)], in0=neg_dg[:], scalar=-1.0, in1=r_sb[h][:, span(j, HALF)], op0=ALU.mult, op1=ALU.mult)
 
         def make_dz1(j, h):
             engine = nc.vector if j == SLOTS[-1] else nc.gpsimd
-            engine.tensor_tensor(out=dz1_sb[h][:, span(j, HALF)], in0=gated[j, h][:], in1=g_sb[j][:, span(h, HALF)], op=ALU.mult)
+            engine.tensor_tensor(out=dz1_sb[h][:, span(j, HALF)], in0=gated[j, h][:], in1=g_sb[h][:, span(j, HALF)], op=ALU.mult)
 
         def add_out0(j, h):
             dst = out0_sb[j][:, span(h, HALF)]
@@ -204,9 +210,8 @@ def tile_joint_gru_pa_v_kernel(tc, joint_h, mgn_h, W_r, W_h, U_r, U_h, b_r, b_h,
         def quantize_dz2(j):
             quantize(dz2_mx[j], slice(None), dz2_feat[j][:], E5M2)
 
-        def quantize_weight(w, q, kpass):
-            key = (w, q // 2, kpass)
-            quantize(weight_mx[key], span(q % 2, QUARTER), weight_feat[key][:, span(q % 2, PACK * QUARTER)], E4M3)
+        def quantize_weight(w, h, kpass):
+            quantize(weight_mx[w, h, kpass], slice(None), weight_feat[w, h, kpass][:], E4M3)
 
         def quantize_dz1_feat(h, pair):
             quantize(dz1_feat_mx[h, pair], slice(None), dz1_feat[h, pair][:], E5M2)
@@ -227,54 +232,57 @@ def tile_joint_gru_pa_v_kernel(tc, joint_h, mgn_h, W_r, W_h, U_r, U_h, b_r, b_h,
         def by_half(fn, first, h):
             return each(fn, first, [h])
 
-        def weight_steps(fn, w, quarters):
-            return each(fn, [w], quarters, PASSES)
+        def weight_banks(fn, w, h, passes):
+            return each(fn, [w], [h], passes, PAIRS)
 
         sync_steps = (
-            [(load_weight, "U_h", 0), (load_dz2_inputs, 0), (load_weight, "U_h", 1)]
-            + each(load_dz2_inputs, SLOTS[1:])
-            + each(load_weight, ["U_h"], [2, 3])
-            + by_half(load_gate, SLOTS, 0)
-            + [(load_joint,)]
-            + each(load_weight, ["U_r"], [0, 1])
-            + by_half(load_gate, SLOTS, 1)
-            + each(load_weight, ["U_r"], [2, 3])
-            + by_half(store_out1, ROW_TILES, 0)
-            + by_half(store_out1, ROW_TILES, 1)
+            [(load_weight, "U_h", 0)]
+            + [(load_y, 0), (load_grad, 0), (load_y, 1), (load_y, 2), (load_grad, 1), (load_y, 3)]
+            + [(load_weight, "U_h", 1)]
+            + by_half(load_gate, PAIRS, 0)
+            + [(load_joint,), (load_weight, "U_r", 0)]
+            + by_half(load_gate, PAIRS, 1)
+            + [(load_weight, "U_r", 1)]
+            + by_half(store_out1, ROW_TILES[::2], 0)
+            + by_half(store_out1, ROW_TILES[::2], 1)
             + each(store_out0, SLOTS)
         )
 
         tensor_steps = (
-            weight_steps(turn_weight, "U_h", [0, 1])
-            + each(turn_dz2, [0, 1])
-            + [(product_dg, 0, 0), (turn_dz2, 2), (turn_weight, "U_h", 2, 0), (turn_dz2, 3), (turn_weight, "U_h", 2, 1)]
+            weight_banks(turn_weight, "U_h", 0, PASSES)
+            + each(turn_dz2, SLOTS[:-1])
+            + [(product_dg, 0, 0), (turn_dz2, SLOTS[-1])]
             + by_half(product_dg, SLOTS[1:], 0)
-            + weight_steps(turn_weight, "U_h", [3])
+            + weight_banks(turn_weight, "U_h", 1, PASSES)
             + each(turn_dz1, [0], PAIRS)
             + by_half(product_dg, SLOTS, 1)
-            + weight_steps(turn_weight, "U_r", [0])
+            + weight_banks(turn_weight, "U_r", 0, [0])
             + by_half(product_out1, ROW_TILES[:2], 0)
-            + weight_steps(turn_weight, "U_r", [1])
+            + weight_banks(turn_weight, "U_r", 0, [1])
             + by_half(product_out1, ROW_TILES[2:], 0)
             + [(turn_dz1, 1, 0)]
-            + weight_steps(turn_weight, "U_r", [2, 3])
+            + weight_banks(turn_weight, "U_r", 1, [0])
             + [(turn_dz1, 1, 1)]
-            + by_half(product_out1, ROW_TILES, 1)
+            + by_half(product_out1, ROW_TILES[:6], 1)
+            + weight_banks(turn_weight, "U_r", 1, [1])
+            + by_half(product_out1, ROW_TILES[6:], 1)
             + each(product_out0, SLOTS, HALVES)
         )
 
         scalar_steps = (
-            [(square, 0), (square, 1), (copy_dz2, 0), (square, 2), (square, 3), (copy_dz2, 1), (copy_dz2, 2)]
-            + [(copy_weight, "U_h", 2, 0), (copy_dz2, 3), (copy_weight, "U_h", 2, 1)]
-            + weight_steps(copy_weight, "U_h", [3])
+            [(square, 0)]
+            + weight_banks(copy_weight, "U_h", 0, [1])
+            + [(square, 1), (square, 2), (copy_dz2, 0), (square, 3)]
+            + each(copy_dz2, SLOTS[1:])
+            + weight_banks(copy_weight, "U_h", 1, PASSES)
             + [(copy_dz1, 0, 0)]
             + each(interleave_joint, QUARTERS[:-1])
             + [(copy_dz1, 0, 1)]
-            + weight_steps(copy_weight, "U_r", [0])
+            + weight_banks(copy_weight, "U_r", 0, [0])
             + by_half(copy_out1, ROW_TILES[:2], 0)
-            + weight_steps(copy_weight, "U_r", [1])
+            + weight_banks(copy_weight, "U_r", 0, [1])
             + by_half(copy_out1, ROW_TILES[2:], 0)
-            + weight_steps(copy_weight, "U_r", [2])
+            + weight_banks(copy_weight, "U_r", 1, [0])
             + by_half(copy_out1, ROW_TILES, 1)
         )
 
@@ -282,17 +290,15 @@ def tile_joint_gru_pa_v_kernel(tc, joint_h, mgn_h, W_r, W_h, U_r, U_h, b_r, b_h,
             return [(fn, j, h) for j in SLOTS for fn in (gate_dg, dg_times_r)] + [(make_dz1, SLOTS[-1], h)]
 
         vector_steps = (
-            weight_steps(copy_weight, "U_h", [0])
+            weight_banks(copy_weight, "U_h", 0, [0])
             + [(neg_dz2, 0)]
-            + weight_steps(quantize_weight, "U_h", [0])
-            + weight_steps(copy_weight, "U_h", [1])
-            + [(neg_dz2, 1)]
-            + weight_steps(quantize_weight, "U_h", [1])
-            + [(quantize_dz2, 0), (neg_dz2, 2), (neg_dz2, 3), (quantize_dz2, 1), (quantize_dz2, 2)]
-            + [(quantize_weight, "U_h", 2, 0), (quantize_dz2, 3)]
-            + read_dg(0)
-            + [(quantize_weight, "U_h", 2, 1)]
-            + weight_steps(quantize_weight, "U_h", [3])
+            + each(quantize_weight, ["U_h"], [0], PASSES)
+            + [(neg_dz2, 1), (neg_dz2, 2), (quantize_dz2, 0), (neg_dz2, 3)]
+            + each(quantize_dz2, SLOTS[1:-1])
+            + read_dg(0)[:2]
+            + [(quantize_dz2, SLOTS[-1])]
+            + read_dg(0)[2:]
+            + each(quantize_weight, ["U_h"], [1], PASSES)
             + each(interleave_dz1, [0], PARTS)
             + [(interleave_joint, QUARTERS[-1])]
             + each(quantize_dz1_tok, [0], PARTS)
@@ -302,10 +308,10 @@ def tile_joint_gru_pa_v_kernel(tc, joint_h, mgn_h, W_r, W_h, U_r, U_h, b_r, b_h,
             + each(interleave_dz1, [1], PARTS)
             + each(quantize_dz1_tok, [1], PARTS)
             + each(copy_dz1, [1], PAIRS)
-            + weight_steps(copy_weight, "U_r", [3])
-            + weight_steps(quantize_weight, "U_r", [0, 1])
+            + each(quantize_weight, ["U_r"], [0], PASSES)
             + each(quantize_dz1_feat, [1], PAIRS)
-            + weight_steps(quantize_weight, "U_r", [2, 3])
+            + weight_banks(copy_weight, "U_r", 1, [1])
+            + each(quantize_weight, ["U_r"], [1], PASSES)
             + each(add_out0, SLOTS, HALVES)
         )
 
@@ -321,20 +327,20 @@ def tile_joint_gru_pa_v_kernel(tc, joint_h, mgn_h, W_r, W_h, U_r, U_h, b_r, b_h,
 
 
         def weight_half(w, h):
-            return weight_steps(quantize_weight, w, [2 * h, 2 * h + 1])
+            return each(quantize_weight, [w], [h], PASSES)
 
         reads = {
-            square: lambda j: [(load_dz2_inputs, j)],
-            neg_dz2: lambda j: [(square, j)],
+            square: lambda j: [(load_y, j)],
+            neg_dz2: lambda j: [(square, j), (load_grad, j // 2)],
             turn_dz2: lambda j: [(neg_dz2, j)],
             copy_dz2: lambda j: [(turn_dz2, j)],
             quantize_dz2: lambda j: [(copy_dz2, j)],
-            turn_weight: lambda w, q, kpass: [(load_weight, w, q)],
-            copy_weight: lambda w, q, kpass: [(turn_weight, w, q, kpass)],
-            quantize_weight: lambda w, q, kpass: [(copy_weight, w, q, kpass)],
+            turn_weight: lambda w, h, kpass, pair: [(load_weight, w, h)],
+            copy_weight: lambda w, h, kpass, pair: [(turn_weight, w, h, kpass, pair)],
+            quantize_weight: lambda w, h, kpass: weight_banks(copy_weight, w, h, [kpass]),
             product_dg: lambda j, h: [(quantize_dz2, j)] + weight_half("U_h", h),
-            gate_dg: lambda j, h: [(load_gate, j, h), (product_dg, j, h)] + each(make_dz1, [j], HALVES[:h]),
-            dg_times_r: lambda j, h: [(load_gate, j, h), (product_dg, j, h)],
+            gate_dg: lambda j, h: [(load_gate, j // 2, h), (product_dg, j, h)] + each(make_dz1, [j], HALVES[:h]),
+            dg_times_r: lambda j, h: [(load_gate, j // 2, h), (product_dg, j, h)],
             make_dz1: lambda j, h: [(gate_dg, j, h)],
             turn_dz1: lambda h, pair: by_half(make_dz1, [2 * pair, 2 * pair + 1], h),
             copy_dz1: lambda h, pair: [(turn_dz1, h, pair)],
@@ -345,7 +351,7 @@ def tile_joint_gru_pa_v_kernel(tc, joint_h, mgn_h, W_r, W_h, U_r, U_h, b_r, b_h,
             quantize_joint: lambda h: each(interleave_joint, [2 * h, 2 * h + 1]),
             product_out1: lambda t, h: [(quantize_joint, t // 4)] + each(quantize_dz1_tok, [h], PARTS),
             copy_out1: lambda t, h: [(product_out1, t, h)],
-            store_out1: lambda t, h: [(copy_out1, t, h)],
+            store_out1: lambda t, h: by_half(copy_out1, [t, t + 1], h),
             product_out0: lambda j, h: each(quantize_dz1_feat, PASSES, [j // 2]) + weight_half("U_r", h),
             add_out0: lambda j, h: [(product_out0, j, h), (dg_times_r, j, h)],
             store_out0: lambda j: each(add_out0, [j], HALVES),

from contextlib import ExitStack

import concourse.mybir as mybir
from concourse.masks import make_identity

B, H = 512, 1024
FLOPS = 3 * 2 * B * H * H
BYTES = 2 * (2 * B * H + 2 * H * H) + 4 * (3 * B * H) + 4 * (B * H + H * H)

F32 = mybir.dt.float32
BF16 = mybir.dt.bfloat16
U32 = mybir.dt.uint32
U8 = mybir.dt.uint8
E4M3 = mybir.dt.float8_e4m3fn_x4
E5M2 = mybir.dt.float8_e5m2_x4
ALU = mybir.AluOpType
ACT = mybir.ActivationFunctionType

P = 128
PACK = 4
HALF = 512
QUARTER = 256
SLOTS = range(PACK)
HALVES = range(2)
PASSES = range(2)
PAIRS = range(2)
PARTS = range(2)
QUARTERS = range(4)
ROW_TILES = range(H // P)
BANKS = 8


def tile_joint_gru_pa_v_kernel(tc, joint_h, mgn_h, W_r, W_h, U_r, U_h, b_r, b_h, r, g, y, grad_out, out_0, out_1):
    nc = tc.nc
    with ExitStack() as ctx:
        keep = ctx.enter_context(tc.tile_pool(name="keep", bufs=1))
        psum = ctx.enter_context(tc.psum_pool(name="psum", bufs=1))
        ctx.enter_context(tc.manual_schedule())

        def sbuf(name, width, dtype, tag=""):
            return keep.tile([P, width], dtype, name=name, tag=tag or name, align_bytes=64)

        def mx_tiles(name, words):
            return sbuf(name + "_codes", words, U32), sbuf(name + "_scales", words, U8)

        def span(n, width):
            return slice(n * width, (n + 1) * width)

        def by_slot(tensor):
            return tensor.rearrange("(p j) w -> p j w", j=PACK)

        def quantize(operand, words, src, fmt):
            nc.vector.quantize_mx(out=operand[0][:, words].bitcast(fmt), scales=operand[1][:, words], in_=src)

        def matmul(acc, lhs, lhs_words, lhs_fmt, rhs, rhs_fmt, start, stop):
            nc.tensor.matmul_mx(
                out=acc[:],
                lhsT=lhs[0][:, lhs_words].bitcast(lhs_fmt),
                lhsT_scale=lhs[1][:, lhs_words],
                rhs=rhs[0][:].bitcast(rhs_fmt),
                rhs_scale=rhs[1][:],
                start=start,
                stop=stop,
            )

        ident = sbuf("ident", P, F32)
        make_identity(nc, ident[:])

        weights = {"U_h": U_h, "U_r": U_r}
        grad_sb = sbuf("grad", PACK * H, BF16)
        y_sb = sbuf("y", PACK * H, F32)
        g_sb = [sbuf("g%d" % h, PACK * HALF, F32) for h in HALVES]
        r_sb = [sbuf("r%d" % h, PACK * HALF, F32) for h in HALVES]
        joint_sb = sbuf("joint", PACK * H, BF16)
        weight_sb = {(w, h): sbuf("%s_%d" % (w, h), PACK * H, BF16) for w in weights for h in HALVES}

        out0_sb = [sbuf("out0_%d" % j, H, F32) for j in SLOTS]
        dz1_sb = [sbuf("dz1_%d" % h, PACK * HALF, BF16) for h in HALVES]

        dz2_feat = [sbuf("dz2_feat%d" % j, H, BF16) for j in SLOTS]
        dz2_mx = [mx_tiles("dz2_%d" % j, 2 * P) for j in SLOTS]
        weight_keys = [(w, h, kpass) for w in weights for h in HALVES for kpass in PASSES]
        weight_feat = {key: sbuf("%s_feat%d%d" % key, PACK * HALF, BF16) for key in weight_keys}
        weight_mx = {key: mx_tiles("%s_%d%d" % key, HALF) for key in weight_keys}
        dz1_feat = {(h, pair): sbuf("dz1_feat%d%d" % (h, pair), H, BF16) for h in HALVES for pair in PAIRS}
        dz1_feat_mx = {(h, pair): mx_tiles("dz1_feat%d%d" % (h, pair), 2 * P) for h in HALVES for pair in PAIRS}
        dz1_tok = [sbuf("dz1_tok%d" % h, PACK * HALF, BF16) for h in HALVES]
        dz1_tok_mx = [mx_tiles("dz1_tok%d" % h, HALF) for h in HALVES]
        joint_tok = [sbuf("joint_tok%d" % h, PACK * HALF, BF16) for h in HALVES]
        joint_mx = [mx_tiles("joint%d" % h, HALF) for h in HALVES]
        gated = {}
        filled = {}


        def load_y(j):
            nc.sync.dma_start(out=y_sb[:, span(j, H)], in_=by_slot(y)[:, j, :])

        def load_grad(pair):
            dst = grad_sb[:, span(pair, 2 * H)].rearrange("p (j w) -> p j w", j=2)
            nc.sync.dma_start(out=dst, in_=by_slot(grad_out)[:, span(pair, 2), :])

        def load_gate(pair, h):
            for dst, src in ((r_sb, r), (g_sb, g)):
                dst = dst[h][:, span(pair, 2 * HALF)].rearrange("p (j w) -> p j w", j=2)
                nc.sync.dma_start(out=dst, in_=by_slot(src)[:, span(pair, 2), span(h, HALF)])

        def load_weight(w, h):
            rows = weights[w][span(h, HALF), :]
            nc.sync.dma_start(out=weight_sb[w, h][:], in_=rows.rearrange("(p m) k -> p (m k)", m=PACK))

        def load_joint():
            nc.sync.dma_start(out=joint_sb[:], in_=joint_h.rearrange("(p j) w -> p (j w)", j=PACK))

        def out1_sb(t, h, tiles):
            stage, first = (y_sb, t) if h == 0 else (g_sb[t // PACK], t % PACK)
            return stage[:, first * HALF : (first + tiles) * HALF]

        def store_out1(t, h):
            dst = out_1[t * P : (t + 2) * P, span(h, HALF)].rearrange("(n p) w -> p n w", p=P)
            nc.sync.dma_start(out=dst, in_=out1_sb(t, h, 2).rearrange("p (n w) -> p n w", n=2))

        def store_out0(j):
            nc.sync.dma_start(out=by_slot(out_0)[:, j, :], in_=out0_sb[j][:])


        def turn(bank, sources):
            turned = psum.tile([P, 2, 2, P], F32, name="turned", tag="bank%d" % bank)
            for n, src in enumerate(sources):
                for u in range(2):
                    nc.tensor.transpose(turned[:, n, u, :], src.bitcast(F32)[:, u : 2 * P : 2], ident[:])
            return turned

        def turn_dz2(j, bank):
            return turn(bank, [grad_sb[:, span(2 * j + kpass, HALF)] for kpass in PASSES])

        def turn_weight(w, h, kpass, pair, bank):
            return turn(bank, [weight_sb[w, h][:, span(2 * m + kpass, HALF)] for m in (2 * pair, 2 * pair + 1)])

        def turn_dz1(h, pair, bank):
            return turn(bank, [dz1_sb[h][:, span(2 * pair + n, HALF)] for n in range(2)])

        def product_dg(j, h, bank):
            acc = psum.tile([P, HALF], F32, name="neg_dg", tag="bank%d" % bank)
            for kpass in PASSES:
                matmul(acc, dz2_mx[j], span(kpass, P), E5M2, weight_mx["U_h", h, kpass], E4M3, kpass == 0, kpass == 1)
            return acc

        def product_out1(t, h, bank):
            acc = psum.tile([P, HALF], F32, name="acc1", tag="bank%d" % bank)
            matmul(acc, joint_mx[t // 4], span(t % 4, P), E4M3, dz1_tok_mx[h], E5M2, True, True)
            return acc

        def product_out0(j, h, bank):
            acc = psum.tile([P, HALF], F32, name="acc0", tag="bank%d" % bank)
            for kpass in PASSES:
                matmul(acc, dz1_feat_mx[kpass, j // 2], span(j % 2, P), E5M2, weight_mx["U_r", h, kpass], E4M3, kpass == 0, kpass == 1)
            return acc


        def copy_dz2(j, copy):
            dst = dz2_feat[j][:].bitcast(F32).rearrange("p (kpass c u) -> p kpass c u", kpass=2, u=2)
            copy(out=dst, in_=filled[turn_dz2, j][:].rearrange("p kpass u c -> p kpass c u"))

        def copy_weight(w, h, kpass, pair, copy):
            dst = weight_feat[w, h, kpass][:].bitcast(F32).rearrange("p (c pair n u) -> p pair c n u", pair=2, n=2, u=2)
            copy(out=dst[:, pair], in_=filled[turn_weight, w, h, kpass, pair][:].rearrange("p n u c -> p c n u"))

        def copy_dz1(h, pair, copy):
            dst = dz1_feat[h, pair][:].bitcast(F32).rearrange("p (n c u) -> p n c u", n=2, u=2)
            copy(out=dst, in_=filled[turn_dz1, h, pair][:].rearrange("p n u c -> p n c u"))

        def copy_out1(t, h, copy):
            copy(out=out1_sb(t, h, 1), in_=filled[product_out1, t, h][:])

        def interleave(copy, dst, src, n):
            src = src.rearrange("p (j w) -> p j w", j=PACK)[:, :, span(n, QUARTER)]
            copy(out=dst.rearrange("p (c i j) -> p c j i", i=4, j=PACK), in_=src.rearrange("p j (c i) -> p c j i", i=4))

        def interleave_dz1(h, part, copy):
            interleave(copy, dz1_tok[h][:, span(part, PACK * QUARTER)], dz1_sb[h][:], part)

        def interleave_joint(q, copy):
            interleave(copy, joint_tok[q // 2][:, span(q % 2, PACK * QUARTER)], joint_sb[:], q)


        def square(j):
            nc.scalar.activation(out=y_sb[:, span(j, H)], in_=y_sb[:, span(j, H)], func=ACT.Square)

        def neg_dz2(j):
            grad = grad_sb[:, span(j, H)]
            nc.vector.scalar_tensor_tensor(out=grad, in0=y_sb[:, span(j, H)], scalar=1.0, in1=grad, op0=ALU.subtract, op1=ALU.mult)

        def gate_dg(j, h):
            gated[j, h] = sbuf("gated", HALF, F32, tag="gated%d" % j)
            neg_dg = filled[product_dg, j, h]
            nc.vector.scalar_tensor_tensor(out=gated[j, h][:], in0=r_sb[h][:, span(j, HALF)], scalar=1.0, in1=neg_dg[:], op0=ALU.subtract, op1=ALU.mult)

        def dg_times_r(j, h):
            neg_dg = filled[product_dg, j, h]
            nc.vector.scalar_tensor_tensor(out=out0_sb[j][:, span(h, HALF)], in0=neg_dg[:], scalar=-1.0, in1=r_sb[h][:, span(j, HALF)], op0=ALU.mult, op1=ALU.mult)

        def make_dz1(j, h):
            engine = nc.vector if j == SLOTS[-1] else nc.gpsimd
            engine.tensor_tensor(out=dz1_sb[h][:, span(j, HALF)], in0=gated[j, h][:], in1=g_sb[h][:, span(j, HALF)], op=ALU.mult)

        def add_out0(j, h):
            dst = out0_sb[j][:, span(h, HALF)]
            nc.vector.tensor_tensor(out=dst, in0=filled[product_out0, j, h][:], in1=dst, op=ALU.add)

        def quantize_dz2(j):
            quantize(dz2_mx[j], slice(None), dz2_feat[j][:], E5M2)

        def quantize_weight(w, h, kpass):
            quantize(weight_mx[w, h, kpass], slice(None), weight_feat[w, h, kpass][:], E4M3)

        def quantize_dz1_feat(h, pair):
            quantize(dz1_feat_mx[h, pair], slice(None), dz1_feat[h, pair][:], E5M2)

        def quantize_dz1_tok(h, part):
            quantize(dz1_tok_mx[h], span(part, QUARTER), dz1_tok[h][:, span(part, PACK * QUARTER)], E5M2)

        def quantize_joint(h):
            quantize(joint_mx[h], slice(None), joint_tok[h][:], E4M3)


        def each(fn, *ranges):
            steps = [(fn,)]
            for values in ranges:
                steps = [step + (value,) for step in steps for value in values]
            return steps

        def by_half(fn, first, h):
            return each(fn, first, [h])

        def weight_banks(fn, w, h, passes):
            return each(fn, [w], [h], passes, PAIRS)

        sync_steps = (
            [(load_weight, "U_h", 0)]
            + [(load_y, 0), (load_grad, 0), (load_y, 1), (load_y, 2), (load_grad, 1), (load_y, 3)]
            + [(load_weight, "U_h", 1)]
            + by_half(load_gate, PAIRS, 0)
            + [(load_joint,), (load_weight, "U_r", 0)]
            + by_half(load_gate, PAIRS, 1)
            + [(load_weight, "U_r", 1)]
            + by_half(store_out1, ROW_TILES[::2], 0)
            + by_half(store_out1, ROW_TILES[::2], 1)
            + each(store_out0, SLOTS)
        )

        tensor_steps = (
            weight_banks(turn_weight, "U_h", 0, PASSES)
            + each(turn_dz2, SLOTS[:-1])
            + [(product_dg, 0, 0), (turn_dz2, SLOTS[-1])]
            + by_half(product_dg, SLOTS[1:], 0)
            + weight_banks(turn_weight, "U_h", 1, PASSES)
            + each(turn_dz1, [0], PAIRS)
            + by_half(product_dg, SLOTS, 1)
            + weight_banks(turn_weight, "U_r", 0, [0])
            + by_half(product_out1, ROW_TILES[:2], 0)
            + weight_banks(turn_weight, "U_r", 0, [1])
            + by_half(product_out1, ROW_TILES[2:], 0)
            + [(turn_dz1, 1, 0)]
            + weight_banks(turn_weight, "U_r", 1, [0])
            + [(turn_dz1, 1, 1)]
            + by_half(product_out1, ROW_TILES[:6], 1)
            + weight_banks(turn_weight, "U_r", 1, [1])
            + by_half(product_out1, ROW_TILES[6:], 1)
            + each(product_out0, SLOTS, HALVES)
        )

        scalar_steps = (
            [(square, 0)]
            + weight_banks(copy_weight, "U_h", 0, [1])
            + [(square, 1), (square, 2), (copy_dz2, 0), (square, 3)]
            + each(copy_dz2, SLOTS[1:])
            + weight_banks(copy_weight, "U_h", 1, PASSES)
            + [(copy_dz1, 0, 0)]
            + each(interleave_joint, QUARTERS[:-1])
            + [(copy_dz1, 0, 1)]
            + weight_banks(copy_weight, "U_r", 0, [0])
            + by_half(copy_out1, ROW_TILES[:2], 0)
            + weight_banks(copy_weight, "U_r", 0, [1])
            + by_half(copy_out1, ROW_TILES[2:], 0)
            + weight_banks(copy_weight, "U_r", 1, [0])
            + by_half(copy_out1, ROW_TILES, 1)
        )

        def read_dg(h):
            return [(fn, j, h) for j in SLOTS for fn in (gate_dg, dg_times_r)] + [(make_dz1, SLOTS[-1], h)]

        vector_steps = (
            weight_banks(copy_weight, "U_h", 0, [0])
            + [(neg_dz2, 0)]
            + each(quantize_weight, ["U_h"], [0], PASSES)
            + [(neg_dz2, 1), (neg_dz2, 2), (quantize_dz2, 0), (neg_dz2, 3)]
            + each(quantize_dz2, SLOTS[1:-1])
            + read_dg(0)[:2]
            + [(quantize_dz2, SLOTS[-1])]
            + read_dg(0)[2:]
            + each(quantize_weight, ["U_h"], [1], PASSES)
            + each(interleave_dz1, [0], PARTS)
            + [(interleave_joint, QUARTERS[-1])]
            + each(quantize_dz1_tok, [0], PARTS)
            + [(quantize_joint, 0), (quantize_dz1_feat, 0, 0), (quantize_joint, 1)]
            + read_dg(1)
            + [(quantize_dz1_feat, 0, 1)]
            + each(interleave_dz1, [1], PARTS)
            + each(quantize_dz1_tok, [1], PARTS)
            + each(copy_dz1, [1], PAIRS)
            + each(quantize_weight, ["U_r"], [0], PASSES)
            + each(quantize_dz1_feat, [1], PAIRS)
            + weight_banks(copy_weight, "U_r", 1, [1])
            + each(quantize_weight, ["U_r"], [1], PASSES)
            + each(add_out0, SLOTS, HALVES)
        )

        gpsimd_steps = by_half(make_dz1, SLOTS[:-1], 0) + by_half(make_dz1, SLOTS[:-1], 1)

        all_banks_from = tensor_steps.index((product_out1, 6, 0))
        early = [step for step in tensor_steps[:all_banks_from] if step[0] != product_dg]
        bank_of = dict(
            [(step, step[1]) for step in tensor_steps if step[0] == product_dg]
            + [(step, PACK + n % (BANKS - PACK)) for n, step in enumerate(early)]
            + [(step, n % BANKS) for n, step in enumerate(tensor_steps[all_banks_from:])]
        )


        def weight_half(w, h):
            return each(quantize_weight, [w], [h], PASSES)

        reads = {
            square: lambda j: [(load_y, j)],
            neg_dz2: lambda j: [(square, j), (load_grad, j // 2)],
            turn_dz2: lambda j: [(neg_dz2, j)],
            copy_dz2: lambda j: [(turn_dz2, j)],
            quantize_dz2: lambda j: [(copy_dz2, j)],
            turn_weight: lambda w, h, kpass, pair: [(load_weight, w, h)],
            copy_weight: lambda w, h, kpass, pair: [(turn_weight, w, h, kpass, pair)],
            quantize_weight: lambda w, h, kpass: weight_banks(copy_weight, w, h, [kpass]),
            product_dg: lambda j, h: [(quantize_dz2, j)] + weight_half("U_h", h),
            gate_dg: lambda j, h: [(load_gate, j // 2, h), (product_dg, j, h)] + each(make_dz1, [j], HALVES[:h]),
            dg_times_r: lambda j, h: [(load_gate, j // 2, h), (product_dg, j, h)],
            make_dz1: lambda j, h: [(gate_dg, j, h)],
            turn_dz1: lambda h, pair: by_half(make_dz1, [2 * pair, 2 * pair + 1], h),
            copy_dz1: lambda h, pair: [(turn_dz1, h, pair)],
            quantize_dz1_feat: lambda h, pair: [(copy_dz1, h, pair)],
            interleave_dz1: lambda h, part: by_half(make_dz1, SLOTS, h),
            quantize_dz1_tok: lambda h, part: [(interleave_dz1, h, part)],
            interleave_joint: lambda q: [(load_joint,)],
            quantize_joint: lambda h: each(interleave_joint, [2 * h, 2 * h + 1]),
            product_out1: lambda t, h: [(quantize_joint, t // 4)] + each(quantize_dz1_tok, [h], PARTS),
            copy_out1: lambda t, h: [(product_out1, t, h)],
            store_out1: lambda t, h: by_half(copy_out1, [t, t + 1], h),
            product_out0: lambda j, h: each(quantize_dz1_feat, PASSES, [j // 2]) + weight_half("U_r", h),
            add_out0: lambda j, h: [(product_out0, j, h), (dg_times_r, j, h)],
            store_out0: lambda j: each(add_out0, [j], HALVES),
        }
        last_reader = {
            turn_dz2: copy_dz2,
            turn_weight: copy_weight,
            turn_dz1: copy_dz1,
            product_dg: dg_times_r,
            product_out1: copy_out1,
            product_out0: add_out0,
        }
        copies = (copy_dz2, copy_weight, copy_dz1, copy_out1, interleave_dz1, interleave_joint)

        waits_for = {}
        bank_freed_by = {}
        for step in tensor_steps:
            waits_for[step] = bank_freed_by.get(bank_of[step], [])
            bank_freed_by[bank_of[step]] = [(last_reader[step[0]],) + step[1:]]

        def ready(step):
            sources = reads[step[0]](*step[1:]) if step[0] in reads else []
            return all(source in written for source in sources + waits_for.get(step, []))

        queues = [
            (sync_steps, None),
            (tensor_steps, None),
            (scalar_steps, nc.scalar.copy),
            (vector_steps, nc.vector.tensor_copy),
            (gpsimd_steps, None),
        ]
        written = set()
        while len(written) < sum(len(steps) for steps, copy in queues):
            before = len(written)
            for steps, copy in queues:
                for step in steps:
                    if step in written:
                        continue
                    if not ready(step):
                        break
                    if step in bank_of:
                        filled[step] = step[0](*step[1:], bank_of[step])
                    elif step[0] in copies:
                        step[0](*step[1:], copy)
                    else:
                        step[0](*step[1:])
                    written.add(step)
            assert len(written) > before, "the queues wait for each other"
